import numpy as np
import ml_dtypes


def mxq(x, axis, fmt="e4m3"):
    dtype, down = {"e4m3": (ml_dtypes.float8_e4m3fn, 7), "e5m2": (ml_dtypes.float8_e5m2, 14)}[fmt]
    v = np.moveaxis(np.asarray(x, np.float32).astype(ml_dtypes.bfloat16).astype(np.float64), axis, -1)
    blocks = v.reshape(v.shape[:-1] + (-1, 32))
    amax = np.abs(blocks).max(-1, keepdims=True)
    byte = np.maximum(np.where(amax > 0, np.frexp(amax)[1] - 1 + 127, 0) - down, 1)
    scale = np.exp2(byte - 127.0)
    codes = (blocks / scale).astype(np.float32).astype(dtype).astype(np.float64)
    return np.moveaxis((codes * scale).reshape(v.shape), -1, axis)


WIDE = False


def mx_kscale(k):
    if not WIDE:
        return np.ones(k)
    levels = np.array([10, -10, 5, -5, 0])
    if k % 512:
        return np.exp2(np.random.permutation(np.resize(levels, k // 32))).repeat(32)
    a = np.empty((k // 512, 16))
    for p in range(k // 512):
        a[p, :8] = np.random.permutation(np.resize(levels, 8))
        for g in range(8):
            far = levels[np.abs(levels - a[p, g]) >= 10]
            a[p, g + 8] = far[np.random.randint(len(far))]
    return np.exp2(a.ravel()).repeat(32)


BF16 = ml_dtypes.bfloat16


def bf(x):
    return np.asarray(x, np.float32).astype(BF16)


def f64(x):
    return np.asarray(x).astype(np.float64)


E2M1 = np.array([0.0, 0.5, 1.0, 1.5, 2.0, 3.0, 4.0, 6.0, -0.0, -0.5, -1.0, -1.5, -2.0, -3.0, -4.0, -6.0])


def pack_weight(w, fmt):
    k, n = w.shape
    w = f64(bf(w)).reshape(k // 32, 32, n)
    amax = np.abs(w).max(1)
    if fmt == "e4m3":
        byte = np.frexp(amax)[1] - 1 + 127 - 7
    else:
        mant, ex = np.frexp(amax / 6.0)
        byte = np.where(mant > 0.5, ex, ex - 1) + 127
    byte = np.clip(np.where(amax > 0, byte, 1), 1, 254)
    scaled = (w * np.exp2(127.0 - byte)[:, None, :]).reshape(k, n).astype(np.float32)
    by_word = np.ascontiguousarray(scaled.reshape(k // 512, 128, 4, n).transpose(0, 1, 3, 2))
    if fmt == "e4m3":
        words = by_word.astype(ml_dtypes.float8_e4m3fn).view(np.uint8)
    else:
        c = by_word.astype(ml_dtypes.float4_e2m1fn).view(np.uint8) & 0xF
        words = c[..., 0::2] | (c[..., 1::2] << 4)
    return np.ascontiguousarray(words), np.ascontiguousarray(byte.astype(np.uint8).reshape(k // 512, 16, n))


def unpack_weight(words, scales, fmt):
    g, p, n, _ = words.shape
    if fmt == "e4m3":
        vals = np.ascontiguousarray(words).view(ml_dtypes.float8_e4m3fn).astype(np.float64)
    else:
        nib = np.empty((g, p, n, 4), np.uint8)
        nib[..., 0::2] = words & 0xF
        nib[..., 1::2] = words >> 4
        vals = E2M1[nib]
    vals = vals * np.repeat(np.exp2(scales.astype(np.float64) - 127.0), 8, axis=1)[..., None]
    return vals.transpose(0, 1, 3, 2).reshape(g * 512, n)
def pack4(w):
    words, scales = pack_weight(w, "e2m1")
    return words.reshape(words.shape[0], 128, -1), scales


def unpack4(words, scales):
    return unpack_weight(words.reshape(words.shape[0], 128, -1, 2), scales, "e2m1")


B, H, W, DIM, HEADS, Q_RANK, KV_RANK, ROPE, NOPE, VDIM = 2, 32, 16, 2048, 4, 512, 1024, 256, 256, 256
S = H * W
EPS = 1e-5


def gn1(y, g, b):
    mu = y.mean(axis=(1, 2), keepdims=True)
    var = ((y - mu) ** 2).mean(axis=(1, 2), keepdims=True)
    return (y - mu) / np.sqrt(var + EPS) * g[None, :, None] + b[None, :, None]


def freqs():
    n = ROPE // 4
    inv = 1.0 / (10000.0 ** (np.arange(n) / n))
    ah = np.arange(H)[:, None] * inv
    aw = np.arange(W)[:, None] * inv
    fh = np.stack([np.sin(ah), np.cos(ah)], -1)
    fw = np.stack([np.sin(aw), np.cos(aw)], -1)
    fh_b = np.broadcast_to(fh[:, None], (H, W, n, 2))
    fw_b = np.broadcast_to(fw[None, :], (H, W, n, 2))
    return np.stack([fh_b, fw_b], axis=3).reshape(S, ROPE // 2, 2)


def rope(u, f):
    up = u.reshape(u.shape[:-1] + (ROPE // 2, 2))
    fr, fi = f[..., 0], f[..., 1]
    rr = up[..., 0] * fr - up[..., 1] * fi
    ri = up[..., 0] * fi + up[..., 1] * fr
    return np.stack([rr, ri], -1).reshape(u.shape)


def draw0():
    s, t = mx_kscale(DIM), mx_kscale(Q_RANK)
    x = bf(np.random.standard_normal((B, DIM, H, W)) * s[None, :, None, None])
    q1_w = np.random.standard_normal((Q_RANK, DIM)) * 0.5 / np.sqrt(DIM) / s[None, :]
    q1_w_words, q1_w_scales = pack4(q1_w.T)
    q1_b = bf(0.2 + 0.1 * np.random.standard_normal(Q_RANK))
    q_gn_g = bf((1.0 + 0.1 * np.random.standard_normal(Q_RANK)) * t)
    q_gn_b = bf(0.1 * np.random.standard_normal(Q_RANK) * t)
    q2_w = np.random.standard_normal((HEADS * (NOPE + ROPE), Q_RANK)) * 1.5 / np.sqrt(Q_RANK) / t[None, :]
    q2_w_words, q2_w_scales = pack4(q2_w.T)
    q2_b = bf(0.1 * np.random.standard_normal(HEADS * (NOPE + ROPE)))
    return {"x": x,
            "q1_w_words": q1_w_words,
            "q1_w_scales": q1_w_scales,
            "q1_b": q1_b,
            "q_gn_g": q_gn_g,
            "q_gn_b": q_gn_b,
            "q2_w_words": q2_w_words,
            "q2_w_scales": q2_w_scales,
            "q2_b": q2_b}


def core(x, q1_w_words, q1_w_scales, q1_b, q_gn_g, q_gn_b, q2_w_words, q2_w_scales, q2_b):
    xs = f64(x).reshape(B, DIM, S)
    y = (unpack4(q1_w_words, q1_w_scales).T @ mxq(xs, 1, "e4m3")) + f64(q1_b)[None, :, None]
    hq = gn1(y, f64(q_gn_g), f64(q_gn_b))
    q = (unpack4(q2_w_words, q2_w_scales).T @ mxq(hq, 1, "e4m3")) + f64(q2_b)[None, :, None]
    q = q.reshape(B, HEADS, NOPE + ROPE, S).transpose(0, 1, 3, 2)
    return np.concatenate([q[..., :NOPE], rope(q[..., NOPE:], freqs())], axis=-1)


def e4m3fn_bytes(y):
    return np.clip(np.asarray(y, np.float64), -448.0, 448.0).astype(np.float32).astype(ml_dtypes.float8_e4m3fn).view(np.uint8)


def e4m3fn_values(b):
    return np.asarray(b, np.uint8).view(ml_dtypes.float8_e4m3fn).astype(np.float64)


def setup_inputs():
    d = draw0()
    x0 = np.asarray(d['x']).astype(np.float64)
    s = (np.max(np.abs(x0), axis=(0, 2, 3), keepdims=True) / 448.0).astype(np.float32)
    out = {}
    for k, v in d.items():
        if k == 'x':
            out['x_bytes'] = e4m3fn_bytes(x0 / s.astype(np.float64))
            out['x_scale'] = s
        else:
            out[k] = v
    return out


def reference(x_bytes, x_scale, q1_w_words, q1_w_scales, q1_b, q_gn_g, q_gn_b, q2_w_words, q2_w_scales, q2_b):
    return core(e4m3fn_values(x_bytes) * x_scale.astype(np.float64), q1_w_words, q1_w_scales, q1_b, q_gn_g, q_gn_b, q2_w_words, q2_w_scales, q2_b)

@@ -1,0 +1,300 @@
+import math
+from contextlib import ExitStack
+
+import concourse.mybir as mybir
+from concourse.masks import make_identity
+
+F32 = mybir.dt.float32
+BF16 = mybir.dt.bfloat16
+I32 = mybir.dt.int32
+U32 = mybir.dt.uint32
+U8 = mybir.dt.uint8
+FP8 = mybir.dt.float8_e4m3fn
+FP8X4 = mybir.dt.float8_e4m3fn_x4
+FP4X4 = mybir.dt.float4_e2m1fn_x4
+ALU = mybir.AluOpType
+ACT = mybir.ActivationFunctionType
+
+P = 128
+B, H, W, DIM, HEADS, Q_RANK = 2, 32, 16, 2048, 4, 512
+S = H * W
+HEAD_DIM = 512
+NOPE = 256
+G = DIM // 512
+T = 4
+EPS = 1e-5
+FLOPS = 2 * B * S * (DIM * Q_RANK + Q_RANK * HEADS * HEAD_DIM)
+
+
+def tile_imagemla_pa_w4_kernel(tc, x_bytes, x_scale, q1_w_words, q1_w_scales, q1_b, q_gn_g, q_gn_b, q2_w_words, q2_w_scales, q2_b, out):
+    nc = tc.nc
+    with ExitStack() as ctx:
+        const = ctx.enter_context(tc.tile_pool(name="const", bufs=1))
+        small = ctx.enter_context(tc.tile_pool(name="small", bufs=2))
+        xin = ctx.enter_context(tc.tile_pool(name="xin", bufs=8))
+        stage = ctx.enter_context(tc.tile_pool(name="stage", bufs=3))
+        keep = ctx.enter_context(tc.tile_pool(name="keep", bufs=8))
+        outs = ctx.enter_context(tc.tile_pool(name="outs", bufs=3))
+        psum = ctx.enter_context(tc.psum_pool(name="psum", bufs=8))
+
+        dummy = const.tile([P, 1], F32, name="dummy")
+        nc.vector.memset(dummy[:], 0.0)
+        nc.scalar.activation(out=dummy[:], in_=dummy[:], func=ACT.Sin)
+
+        xs = const.tile([P, G, T], F32, name="xs")
+        nc.sync.dma_start(out=xs[:], in_=x_scale.rearrange("a (g p t) c d -> p (a g) (t c d)", p=P, t=T))
+        x_rows = x_bytes.rearrange("b (g p t) h w -> b g p (t h w)", p=P, t=T)
+        xb = {}
+
+        def load_x(b, g):
+            tile = xin.tile([P, T * S], U8, name="xb")
+            nc.sync.dma_start(out=tile[:], in_=x_rows[b, g])
+            xb[b, g] = tile
+
+        load_x(0, 0)
+        w1_raw = const.tile([P, G, 2 * Q_RANK], U8, name="w1_raw", align_bytes=64)
+        nc.sync.dma_start(out=w1_raw[:], in_=q1_w_words.rearrange("g p n -> p g n"))
+        s1_raw = const.tile([P, G, Q_RANK], U8, name="s1_raw", align_bytes=64)
+        nc.vector.memset(s1_raw[:].rearrange("p g n -> p (g n)").bitcast(I32), 0)
+        s2 = const.tile([P, HEADS * HEAD_DIM], U8, name="s2", align_bytes=64)
+        nc.vector.memset(s2[:].bitcast(I32), 0)
+        s1_view = s1_raw[:].rearrange("p g n -> p (g n)").bitcast(I32).rearrange("p (g n) -> p g n", g=G)
+        for q in range(4):
+            nc.sync.dma_start(out=s1_view[32 * q : 32 * q + 4], in_=q1_w_scales.bitcast(I32)[:, 4 * q : 4 * q + 4, :].rearrange("g r n -> r g n"))
+        for g in range(1, G):
+            load_x(0, g)
+        vecs = {}
+        for name, ap in (("q1_b", q1_b), ("q_gn_g", q_gn_g), ("q_gn_b", q_gn_b)):
+            v = const.tile([P, T], BF16, name="v_" + name)
+            nc.sync.dma_start(out=v[:], in_=ap.rearrange("(p t) -> p t", t=T))
+            vecs[name] = v
+        for g in range(G):
+            load_x(1, g)
+        w2 = const.tile([P, 2 * HEADS * HEAD_DIM], U8, name="w2", align_bytes=64)
+        nc.sync.dma_start(out=w2[:], in_=q2_w_words[0])
+        for q in range(4):
+            nc.sync.dma_start(out=s2[32 * q : 32 * q + 4, :].bitcast(I32), in_=q2_w_scales.bitcast(I32)[0, 4 * q : 4 * q + 4, :])
+        qb = const.tile([P, HEADS * HEAD_DIM], BF16, name="qb")
+        nc.sync.dma_start(out=qb[:], in_=q2_b.partition_broadcast(P))
+
+        ident = const.tile([P, P], F32, name="ident")
+        make_identity(nc, ident[:])
+        swap = const.tile([P, P], F32, name="swap")
+        ident_pairs = ident[:].rearrange("p (m e) -> p m e", e=2)
+        swap_pairs = swap[:].rearrange("p (m e) -> p m e", e=2)
+        for e in range(2):
+            nc.gpsimd.tensor_copy(out=swap_pairs[:, :, e], in_=ident_pairs[:, :, 1 - e])
+        ones = const.tile([P, P], F32, name="ones")
+        nc.gpsimd.memset(ones[:], 1.0 / P)
+        ones_bf = const.tile([P, 2], BF16, name="ones_bf")
+        nc.gpsimd.memset(ones_bf[:], 1.0 / P)
+        mhalf = const.tile([P, 1], F32, name="mhalf")
+        nc.gpsimd.memset(mhalf[:], -0.5)
+
+        part = const.tile([P, 1], I32, name="part")
+        nc.gpsimd.iota(part[:], pattern=[[0, 1]], base=0, channel_multiplier=1)
+        pos = const.tile([P, H + W], F32, name="pos")
+        nc.gpsimd.iota(pos[:, 0:H], pattern=[[1, H]], base=0, channel_multiplier=0, allow_small_or_imprecise_dtypes=True)
+        nc.gpsimd.iota(pos[:, H : H + W], pattern=[[1, W]], base=0, channel_multiplier=0, allow_small_or_imprecise_dtypes=True)
+        bits_i = const.tile([P, 3], I32, name="bits_i")
+        nc.vector.tensor_scalar(out=bits_i[:, 0:1], in0=part[:], scalar1=2, scalar2=None, op0=ALU.arith_shift_right)
+        nc.vector.tensor_scalar(out=bits_i[:, 1:2], in0=part[:], scalar1=1, scalar2=1, op0=ALU.arith_shift_right, op1=ALU.bitwise_and)
+        nc.vector.tensor_scalar(out=bits_i[:, 2:3], in0=part[:], scalar1=1, scalar2=None, op0=ALU.bitwise_and)
+        bits = const.tile([P, 3], F32, name="bits")
+        nc.vector.tensor_copy(out=bits[:], in_=bits_i[:])
+        expo = const.tile([P, 2], F32, name="expo")
+        for dt in range(2):
+            nc.vector.tensor_scalar(out=expo[:, dt : dt + 1], in0=bits[:, 0:1], scalar1=32.0 * dt, scalar2=-1.0 / 64, op0=ALU.add, op1=ALU.mult)
+        base = const.tile([P, 2], F32, name="base")
+        nc.gpsimd.memset(base[:], 10000.0)
+        inv = const.tile([P, 2], F32, name="inv")
+        nc.gpsimd.tensor_tensor(out=inv[:], in0=base[:], in1=expo[:], op=ALU.pow)
+        turn_step = const.tile([P, 2], F32, name="turn_step")
+        nc.vector.tensor_scalar(out=turn_step[:], in0=inv[:], scalar1=1.0 / (2 * math.pi), scalar2=None, op0=ALU.mult)
+        factor = const.tile([P, 2, 2], F32, name="factor")
+        nc.vector.tensor_scalar(out=factor[:, 0, 0:1], in0=bits[:, 1:2], scalar1=-1.0, scalar2=1.0, op0=ALU.mult, op1=ALU.add)
+        nc.vector.tensor_copy(out=factor[:, 0, 1:2], in_=bits[:, 1:2])
+        sign = const.tile([P, 1], F32, name="sign")
+        nc.vector.tensor_scalar(out=sign[:], in0=bits[:, 2:3], scalar1=-2.0, scalar2=1.0, op0=ALU.mult, op1=ALU.add)
+        nc.vector.tensor_scalar(out=factor[:, 1, :], in0=factor[:, 0, :], scalar1=sign[:], scalar2=None, op0=ALU.mult)
+
+        turns = const.tile([P, 2, 2, H + W], F32, name="turns")
+        for dt in range(2):
+            nc.vector.tensor_scalar(out=turns[:, dt, 0, :], in0=pos[:], scalar1=turn_step[:, dt : dt + 1], scalar2=None, op0=ALU.mult)
+            nc.vector.tensor_scalar(out=turns[:, dt, 1, :], in0=pos[:], scalar1=turn_step[:, dt : dt + 1], scalar2=0.25, op0=ALU.mult, op1=ALU.add)
+        turns_flat = turns[:].rearrange("p d k n -> p (d k n)")
+        whole = const.tile([P, 4 * (H + W)], I32, name="whole")
+        nc.vector.tensor_copy(out=whole[:], in_=turns_flat)
+        frac = const.tile([P, 4 * (H + W)], F32, name="frac")
+        nc.vector.tensor_tensor(out=frac[:], in0=turns_flat, in1=whole[:], op=ALU.subtract)
+        wrapped = const.tile([P, 2, 2, H + W], F32, name="wrapped")
+        nc.vector.scalar_tensor_tensor(out=wrapped[:].rearrange("p d k n -> p (d k n)"), in0=frac[:], scalar=0.5, in1=frac[:], op0=ALU.is_gt, op1=ALU.subtract)
+        masked = const.tile([P, 2, 2, H + W], F32, name="masked")
+        for k in range(2):
+            for axis, cols in ((0, slice(0, H)), (1, slice(H, H + W))):
+                nc.vector.tensor_scalar(out=masked[:, :, k, cols], in0=wrapped[:, :, k, cols], scalar1=factor[:, k, axis : axis + 1], scalar2=None, op0=ALU.mult)
+        waves = const.tile([P, 4, H + W], F32, name="waves")
+        nc.scalar.activation(out=waves[:].rearrange("p k n -> p (k n)"), in_=masked[:].rearrange("p d k n -> p (d k n)"), func=ACT.Sin, scale=-2 * math.pi)
+        table = const.tile([P, 4, S], F32, name="table")
+        for k in range(4):
+            nc.vector.tensor_tensor(
+                out=table[:, k, :].rearrange("p (h w) -> p h w", h=H),
+                in0=waves[:, k, 0:H].unsqueeze(2).to_broadcast([P, H, W]),
+                in1=waves[:, k, H : H + W].unsqueeze(1).to_broadcast([P, H, W]),
+                op=ALU.add,
+            )
+
+        w1 = const.tile([P, G, 2 * Q_RANK], U8, name="w1", align_bytes=64)
+        s1 = const.tile([P, G, Q_RANK], U8, name="s1", align_bytes=64)
+
+        def permute(g):
+            nc.vector.tensor_copy(out=w1[:, g, :].rearrange("p (t m e) -> p t m e", t=T, e=2), in_=w1_raw[:, g, :].rearrange("p (m t e) -> p t m e", t=T, e=2))
+            nc.vector.tensor_copy(out=s1[:, g, :].rearrange("p (t m) -> p t m", t=T), in_=s1_raw[:, g, :].rearrange("p (m t) -> p t m", t=T))
+
+        gb = const.tile([P, 3, T], F32, name="gb")
+        for i, name in enumerate(("q1_b", "q_gn_g", "q_gn_b")):
+            nc.gpsimd.tensor_copy(out=gb[:, i, :], in_=vecs[name][:])
+
+        x_codes = {}
+
+        def quantize_x(b, g):
+            wide = stage.tile([P, T, S], BF16, name="wide")
+            for t in range(T):
+                nc.scalar.activation(out=wide[:, t, :], in_=xb[b, g][:, t * S : (t + 1) * S].bitcast(FP8), func=ACT.Copy, scale=xs[:, g, t : t + 1])
+            quads = stage.tile([P, S, T], BF16, name="quads", align_bytes=64)
+            nc.vector.tensor_copy(out=quads[:], in_=wide[:].rearrange("p t n -> p n t"))
+            codes = keep.tile([P, S], U32, name="codes", align_bytes=64)
+            scales = keep.tile([P, S], U8, name="scales", align_bytes=64)
+            nc.vector.quantize_mx(out=codes[:].bitcast(FP8X4), scales=scales[:], in_=quads[:].rearrange("p n t -> p (n t)"))
+            x_codes[b, g] = (codes, scales)
+
+        y = {}
+
+        def first_matmul(b, g):
+            codes, scales = x_codes[b, g]
+            for t in range(T):
+                if g == 0:
+                    y[b, t] = psum.tile([P, S], F32, name="bank")
+                nc.tensor.matmul_mx(
+                    out=y[b, t][:],
+                    lhsT=w1[:, g, 256 * t : 256 * (t + 1)].bitcast(FP4X4),
+                    lhsT_scale=s1[:, g, P * t : P * (t + 1)],
+                    rhs=codes[:].bitcast(FP8X4),
+                    rhs_scale=scales[:],
+                    start=(g == 0),
+                    stop=(g == G - 1),
+                )
+
+        h_codes = {}
+
+        def normalise(b):
+            st = small.tile([P, T, 2, 3], F32, name="st")
+            for t in range(T):
+                nc.vector.bn_stats(out=st[:, t].rearrange("p a b -> p (a b)"), in_=y[b, t][:])
+            nc.vector.tensor_tensor(out=st[:, :, :, 1], in0=st[:, :, :, 1], in1=gb[:, 0, :].unsqueeze(2).to_broadcast([P, T, 2]), op=ALU.add)
+            ag = small.tile([P, 2], F32, name="ag")
+            nc.vector.bn_aggr(out=ag[:], in_=st[:].rearrange("p t a b -> p (t a b)"))
+            nc.vector.scalar_tensor_tensor(out=ag[:, 1:2], in0=ag[:, 0:1], scalar=ag[:, 0:1], in1=ag[:, 1:2], op0=ALU.mult, op1=ALU.add)
+            tot = psum.tile([P, S], F32, name="bank")
+            nc.tensor.matmul(tot[:, 0:2], lhsT=ones[:], rhs=ag[:], start=True, stop=True)
+            mu = small.tile([P, 2], F32, name="mu")
+            nc.vector.tensor_copy(out=mu[:], in_=tot[:, 0:2])
+            nvar = small.tile([P, 1], F32, name="nvar")
+            nc.vector.scalar_tensor_tensor(out=nvar[:], in0=mu[:, 0:1], scalar=mu[:, 0:1], in1=mu[:, 1:2], op0=ALU.mult, op1=ALU.subtract)
+            nc.vector.tensor_scalar(out=nvar[:], in0=nvar[:], scalar1=-1.0, scalar2=EPS, op0=ALU.mult, op1=ALU.add)
+            rstd = small.tile([P, 1], F32, name="rstd")
+            nc.gpsimd.tensor_tensor(out=rstd[:], in0=nvar[:], in1=mhalf[:], op=ALU.pow)
+            sc = small.tile([P, T], F32, name="sc")
+            nc.vector.tensor_scalar(out=sc[:], in0=gb[:, 1, :], scalar1=rstd[:], scalar2=None, op0=ALU.mult)
+            bi = small.tile([P, T], F32, name="bi")
+            nc.vector.scalar_tensor_tensor(out=bi[:], in0=gb[:, 0, :], scalar=mu[:, 0:1], in1=sc[:], op0=ALU.subtract, op1=ALU.mult)
+            nc.vector.tensor_tensor(out=bi[:], in0=bi[:], in1=gb[:, 2, :], op=ALU.add)
+            hw = stage.tile([P, T, S], BF16, name="hw", bufs=2)
+            for t in range(T):
+                nc.scalar.activation(out=hw[:, t, :], in_=y[b, t][:], func=ACT.Identity, scale=sc[:, t : t + 1], bias=bi[:, t : t + 1])
+            hq = stage.tile([P, S, T], BF16, name="hq", align_bytes=64, bufs=2)
+            nc.vector.tensor_copy(out=hq[:], in_=hw[:].rearrange("p t n -> p n t"))
+            codes = keep.tile([P, S], U32, name="hcodes", align_bytes=64, bufs=2)
+            scales = keep.tile([P, S], U8, name="hscales", align_bytes=64, bufs=2)
+            nc.vector.quantize_mx(out=codes[:].bitcast(FP8X4), scales=scales[:], in_=hq[:].rearrange("p n t -> p (n t)"))
+            h_codes[b] = (codes, scales)
+
+        b2 = const.tile([P, 2 * HEADS], F32, name="b2")
+
+        def bias_columns():
+            cols = psum.tile([P, S], F32, name="bank")
+            for i in range(2 * HEADS):
+                first = HEAD_DIM * (i // 2) + NOPE + P * (i % 2)
+                nc.tensor.matmul(cols[:, i : i + 1], lhsT=qb[:, first : first + P], rhs=ones_bf[:, 0:1], start=True, stop=True)
+            nc.vector.tensor_copy(out=b2[:], in_=cols[:, 0 : 2 * HEADS])
+
+        def head(b, h):
+            codes, scales = h_codes[b]
+            result = outs.tile([P, 4, HEAD_DIM], F32, name="result")
+            products = []
+            for dt in range(2):
+                first = HEAD_DIM * h + NOPE + P * dt
+                z = psum.tile([P, S], F32, name="bank")
+                nc.tensor.matmul_mx(
+                    out=z[:],
+                    lhsT=w2[:, 2 * first : 2 * (first + P)].bitcast(FP4X4),
+                    lhsT_scale=s2[:, first : first + P],
+                    rhs=codes[:].bitcast(FP8X4),
+                    rhs_scale=scales[:],
+                    start=True,
+                    stop=True,
+                )
+                bias = b2[:, 2 * h + dt : 2 * h + dt + 1]
+                if dt == 1:
+                    u = stage.tile([P, S], F32, name="u", bufs=3)
+                    nc.scalar.activation(out=u[:], in_=z[:], func=ACT.Identity, bias=bias)
+                for k in range(2):
+                    prod = stage.tile([P, S], F32, name="prod", bufs=12)
+                    if dt == 1:
+                        nc.gpsimd.tensor_tensor(out=prod[:], in0=u[:], in1=table[:, 2 * dt + k, :], op=ALU.mult)
+                    else:
+                        nc.vector.scalar_tensor_tensor(out=prod[:], in0=z[:], scalar=bias, in1=table[:, 2 * dt + k, :], op0=ALU.add, op1=ALU.mult)
+                    products.append(prod)
+            for half in range(2):
+                n = psum.tile([P, S], F32, name="bank")
+                for i in range(2):
+                    st = 2 * half + i
+                    nc.tensor.matmul_mx(
+                        out=n[:, NOPE * i : NOPE * (i + 1)],
+                        lhsT=codes[:, P * st : P * (st + 1)].bitcast(FP8X4),
+                        lhsT_scale=scales[:, P * st : P * (st + 1)],
+                        rhs=w2[:, 2 * HEAD_DIM * h : 2 * (HEAD_DIM * h + NOPE)].bitcast(FP4X4),
+                        rhs_scale=s2[:, HEAD_DIM * h : HEAD_DIM * h + NOPE],
+                        start=True,
+                        stop=True,
+                    )
+                nc.vector.tensor_tensor(
+                    out=result[:, 2 * half : 2 * half + 2, 0:NOPE],
+                    in0=n[:].rearrange("p (i d) -> p i d", i=2),
+                    in1=qb[:, HEAD_DIM * h : HEAD_DIM * h + NOPE].unsqueeze(1).to_broadcast([P, 2, NOPE]),
+                    op=ALU.add,
+                )
+            for half in range(2):
+                o = psum.tile([P, S], F32, name="bank")
+                for i in range(2):
+                    st = 2 * half + i
+                    for dt in range(2):
+                        dst = o[:, NOPE * i + P * dt : NOPE * i + P * (dt + 1)]
+                        nc.tensor.matmul(dst, lhsT=products[2 * dt][:, P * st : P * (st + 1)], rhs=ident[:], is_transpose=True, start=True, stop=False)
+                        nc.tensor.matmul(dst, lhsT=products[2 * dt + 1][:, P * st : P * (st + 1)], rhs=swap[:], is_transpose=True, start=False, stop=True)
+                nc.scalar.copy(out=result[:, 2 * half : 2 * half + 2, NOPE:HEAD_DIM], in_=o[:].rearrange("p (i d) -> p i d", i=2))
+                nc.sync.dma_start(out=out[b, h].rearrange("(s p) d -> p s d", p=P)[:, 2 * half : 2 * half + 2], in_=result[:, 2 * half : 2 * half + 2])
+
+        for g in range(G):
+            permute(g)
+            quantize_x(0, g)
+            first_matmul(0, g)
+        normalise(0)
+        for g in range(G):
+            quantize_x(1, g)
+            first_matmul(1, g)
+        normalise(1)
+        bias_columns()
+        for b in range(B):
+            for h in range(HEADS):
+                head(b, h)

@@ -23,6 +23,7 @@ NOPE = 256
 G = DIM // 512
 T = 4
 EPS = 1e-5
+PILED = {(1, 1), (1, 3)}
 FLOPS = 2 * B * S * (DIM * Q_RANK + Q_RANK * HEADS * HEAD_DIM)
 
 
@@ -32,11 +33,12 @@ def tile_imagemla_pa_w4_kernel(tc, x_bytes, x_scale, q1_w_words, q1_w_scales, q1
         const = ctx.enter_context(tc.tile_pool(name="const", bufs=1))
         small = ctx.enter_context(tc.tile_pool(name="small", bufs=2))
         xin = ctx.enter_context(tc.tile_pool(name="xin", bufs=8))
-        stage = ctx.enter_context(tc.tile_pool(name="stage", bufs=3))
+        stage = ctx.enter_context(tc.tile_pool(name="stage", bufs=4))
         keep = ctx.enter_context(tc.tile_pool(name="keep", bufs=8))
         outs = ctx.enter_context(tc.tile_pool(name="outs", bufs=3))
         psum = ctx.enter_context(tc.psum_pool(name="psum", bufs=8))
 
+        ctx.enter_context(tc.manual_schedule())
         dummy = const.tile([P, 1], F32, name="dummy")
         nc.vector.memset(dummy[:], 0.0)
         nc.scalar.activation(out=dummy[:], in_=dummy[:], func=ACT.Sin)
@@ -77,22 +79,13 @@ def tile_imagemla_pa_w4_kernel(tc, x_bytes, x_scale, q1_w_words, q1_w_scales, q1
         qb = const.tile([P, HEADS * HEAD_DIM], BF16, name="qb")
         nc.sync.dma_start(out=qb[:], in_=q2_b.partition_broadcast(P))
 
-        ident = const.tile([P, P], F32, name="ident")
-        make_identity(nc, ident[:])
-        swap = const.tile([P, P], F32, name="swap")
-        ident_pairs = ident[:].rearrange("p (m e) -> p m e", e=2)
-        swap_pairs = swap[:].rearrange("p (m e) -> p m e", e=2)
-        for e in range(2):
-            nc.gpsimd.tensor_copy(out=swap_pairs[:, :, e], in_=ident_pairs[:, :, 1 - e])
-        ones = const.tile([P, P], F32, name="ones")
-        nc.gpsimd.memset(ones[:], 1.0 / P)
-        ones_bf = const.tile([P, 2], BF16, name="ones_bf")
-        nc.gpsimd.memset(ones_bf[:], 1.0 / P)
-        mhalf = const.tile([P, 1], F32, name="mhalf")
-        nc.gpsimd.memset(mhalf[:], -0.5)
 
         part = const.tile([P, 1], I32, name="part")
         nc.gpsimd.iota(part[:], pattern=[[0, 1]], base=0, channel_multiplier=1)
+        first_m = const.tile([P, 2], F32, name="first_m")
+        nc.gpsimd.iota(first_m[:], pattern=[[32, 2]], base=0, channel_multiplier=0, allow_small_or_imprecise_dtypes=True)
+        base = const.tile([P, 2], F32, name="base")
+        nc.gpsimd.memset(base[:], 10000.0)
         pos = const.tile([P, H + W], F32, name="pos")
         nc.gpsimd.iota(pos[:, 0:H], pattern=[[1, H]], base=0, channel_multiplier=0, allow_small_or_imprecise_dtypes=True)
         nc.gpsimd.iota(pos[:, H : H + W], pattern=[[1, W]], base=0, channel_multiplier=0, allow_small_or_imprecise_dtypes=True)
@@ -103,40 +96,64 @@ def tile_imagemla_pa_w4_kernel(tc, x_bytes, x_scale, q1_w_words, q1_w_scales, q1
         bits = const.tile([P, 3], F32, name="bits")
         nc.vector.tensor_copy(out=bits[:], in_=bits_i[:])
         expo = const.tile([P, 2], F32, name="expo")
-        for dt in range(2):
-            nc.vector.tensor_scalar(out=expo[:, dt : dt + 1], in0=bits[:, 0:1], scalar1=32.0 * dt, scalar2=-1.0 / 64, op0=ALU.add, op1=ALU.mult)
-        base = const.tile([P, 2], F32, name="base")
-        nc.gpsimd.memset(base[:], 10000.0)
+        nc.vector.tensor_scalar(out=expo[:], in0=first_m[:], scalar1=bits[:, 0:1], scalar2=-1.0 / 64, op0=ALU.add, op1=ALU.mult)
         inv = const.tile([P, 2], F32, name="inv")
         nc.gpsimd.tensor_tensor(out=inv[:], in0=base[:], in1=expo[:], op=ALU.pow)
-        turn_step = const.tile([P, 2], F32, name="turn_step")
-        nc.vector.tensor_scalar(out=turn_step[:], in0=inv[:], scalar1=1.0 / (2 * math.pi), scalar2=None, op0=ALU.mult)
         factor = const.tile([P, 2, 2], F32, name="factor")
-        nc.vector.tensor_scalar(out=factor[:, 0, 0:1], in0=bits[:, 1:2], scalar1=-1.0, scalar2=1.0, op0=ALU.mult, op1=ALU.add)
-        nc.vector.tensor_copy(out=factor[:, 0, 1:2], in_=bits[:, 1:2])
         sign = const.tile([P, 1], F32, name="sign")
+        nc.vector.tensor_scalar(out=factor[:, 0, 0:1], in0=bits[:, 1:2], scalar1=-1.0, scalar2=1.0, op0=ALU.mult, op1=ALU.add)
         nc.vector.tensor_scalar(out=sign[:], in0=bits[:, 2:3], scalar1=-2.0, scalar2=1.0, op0=ALU.mult, op1=ALU.add)
+        nc.vector.tensor_copy(out=factor[:, 0, 1:2], in_=bits[:, 1:2])
         nc.vector.tensor_scalar(out=factor[:, 1, :], in0=factor[:, 0, :], scalar1=sign[:], scalar2=None, op0=ALU.mult)
-
         turns = const.tile([P, 2, 2, H + W], F32, name="turns")
-        for dt in range(2):
-            nc.vector.tensor_scalar(out=turns[:, dt, 0, :], in0=pos[:], scalar1=turn_step[:, dt : dt + 1], scalar2=None, op0=ALU.mult)
-            nc.vector.tensor_scalar(out=turns[:, dt, 1, :], in0=pos[:], scalar1=turn_step[:, dt : dt + 1], scalar2=0.25, op0=ALU.mult, op1=ALU.add)
-        turns_flat = turns[:].rearrange("p d k n -> p (d k n)")
         whole = const.tile([P, 4 * (H + W)], I32, name="whole")
-        nc.vector.tensor_copy(out=whole[:], in_=turns_flat)
         frac = const.tile([P, 4 * (H + W)], F32, name="frac")
-        nc.vector.tensor_tensor(out=frac[:], in0=turns_flat, in1=whole[:], op=ALU.subtract)
         wrapped = const.tile([P, 2, 2, H + W], F32, name="wrapped")
-        nc.vector.scalar_tensor_tensor(out=wrapped[:].rearrange("p d k n -> p (d k n)"), in0=frac[:], scalar=0.5, in1=frac[:], op0=ALU.is_gt, op1=ALU.subtract)
         masked = const.tile([P, 2, 2, H + W], F32, name="masked")
-        for k in range(2):
-            for axis, cols in ((0, slice(0, H)), (1, slice(H, H + W))):
-                nc.vector.tensor_scalar(out=masked[:, :, k, cols], in0=wrapped[:, :, k, cols], scalar1=factor[:, k, axis : axis + 1], scalar2=None, op0=ALU.mult)
         waves = const.tile([P, 4, H + W], F32, name="waves")
-        nc.scalar.activation(out=waves[:].rearrange("p k n -> p (k n)"), in_=masked[:].rearrange("p d k n -> p (d k n)"), func=ACT.Sin, scale=-2 * math.pi)
         table = const.tile([P, 4, S], F32, name="table")
-        for k in range(4):
+
+        ident = const.tile([P, P], F32, name="ident")
+        make_identity(nc, ident[:])
+        ones = const.tile([P, P], F32, name="ones")
+        nc.gpsimd.memset(ones[:], 1.0 / P)
+        ones_bf = const.tile([P, 2], BF16, name="ones_bf")
+        nc.gpsimd.memset(ones_bf[:], 1.0 / P)
+        mhalf = const.tile([P, 1], F32, name="mhalf")
+        nc.gpsimd.memset(mhalf[:], -0.5)
+        swap = const.tile([P, P], F32, name="swap")
+        ident_pairs = ident[:].rearrange("p (m e) -> p m e", e=2)
+        swap_pairs = swap[:].rearrange("p (m e) -> p m e", e=2)
+        for e in range(2):
+            nc.gpsimd.tensor_copy(out=swap_pairs[:, :, e], in_=ident_pairs[:, :, 1 - e])
+        ident_bf = const.tile([P, P], BF16, name="ident_bf")
+        nc.gpsimd.tensor_copy(out=ident_bf[:], in_=ident[:])
+        gb = const.tile([P, 3, T], F32, name="gb")
+        for i, name in enumerate(("q1_b", "q_gn_g", "q_gn_b")):
+            nc.gpsimd.tensor_copy(out=gb[:, i, :], in_=vecs[name][:])
+
+        w1 = const.tile([P, G, 2 * Q_RANK], U8, name="w1", align_bytes=64)
+        s1 = const.tile([P, G, Q_RANK], U8, name="s1", align_bytes=64)
+        b2 = const.tile([P, 2 * HEADS], F32, name="b2")
+        wide, quads, x_codes, y, stats, hw, hq, h_codes, z, u, prods, result, n_bank = {}, {}, {}, {}, {}, {}, {}, {}, {}, {}, {}, {}, {}
+        half_done = set()
+
+        def angles():
+            for dt in range(2):
+                nc.vector.tensor_scalar(out=turns[:, dt, 0, :], in0=pos[:], scalar1=inv[:, dt : dt + 1], scalar2=1.0 / (2 * math.pi), op0=ALU.mult, op1=ALU.mult)
+            nc.vector.tensor_scalar(out=turns[:, :, 1, :], in0=turns[:, :, 0, :], scalar1=0.25, scalar2=None, op0=ALU.add)
+            turns_flat = turns[:].rearrange("p d k n -> p (d k n)")
+            nc.vector.tensor_copy(out=whole[:], in_=turns_flat)
+            nc.vector.tensor_tensor(out=frac[:], in0=turns_flat, in1=whole[:], op=ALU.subtract)
+            nc.vector.scalar_tensor_tensor(out=wrapped[:].rearrange("p d k n -> p (d k n)"), in0=frac[:], scalar=0.5, in1=frac[:], op0=ALU.is_gt, op1=ALU.subtract)
+            for k in range(2):
+                for axis, cols in ((0, slice(0, H)), (1, slice(H, H + W))):
+                    nc.vector.tensor_scalar(out=masked[:, :, k, cols], in0=wrapped[:, :, k, cols], scalar1=factor[:, k, axis : axis + 1], scalar2=None, op0=ALU.mult)
+
+        def sines():
+            nc.scalar.activation(out=waves[:].rearrange("p k n -> p (k n)"), in_=masked[:].rearrange("p d k n -> p (d k n)"), func=ACT.Sin, scale=-2 * math.pi)
+
+        def tabx(k):
             nc.vector.tensor_tensor(
                 out=table[:, k, :].rearrange("p (h w) -> p h w", h=H),
                 in0=waves[:, k, 0:H].unsqueeze(2).to_broadcast([P, H, W]),
@@ -144,33 +161,44 @@ def tile_imagemla_pa_w4_kernel(tc, x_bytes, x_scale, q1_w_words, q1_w_scales, q1
                 op=ALU.add,
             )
 
-        w1 = const.tile([P, G, 2 * Q_RANK], U8, name="w1", align_bytes=64)
-        s1 = const.tile([P, G, Q_RANK], U8, name="s1", align_bytes=64)
-
-        def permute(g):
+        def perm(g):
             nc.vector.tensor_copy(out=w1[:, g, :].rearrange("p (t m e) -> p t m e", t=T, e=2), in_=w1_raw[:, g, :].rearrange("p (m t e) -> p t m e", t=T, e=2))
             nc.vector.tensor_copy(out=s1[:, g, :].rearrange("p (t m) -> p t m", t=T), in_=s1_raw[:, g, :].rearrange("p (m t) -> p t m", t=T))
 
-        gb = const.tile([P, 3, T], F32, name="gb")
-        for i, name in enumerate(("q1_b", "q_gn_g", "q_gn_b")):
-            nc.gpsimd.tensor_copy(out=gb[:, i, :], in_=vecs[name][:])
+        def widen(b, g, t, on_vector=False):
+            if t == 0:
+                wide[b, g] = stage.tile([P, T, S], BF16, name="wide", bufs=8)
+            src = xb[b, g][:, t * S : (t + 1) * S].bitcast(FP8)
+            if on_vector:
+                nc.vector.tensor_scalar(out=wide[b, g][:, t, :], in0=src, scalar1=xs[:, g, t : t + 1], scalar2=None, op0=ALU.mult)
+            else:
+                nc.scalar.activation(out=wide[b, g][:, t, :], in_=src, func=ACT.Copy, scale=xs[:, g, t : t + 1])
 
-        x_codes = {}
+        def pile(src, dst):
+            banks = []
+            for i in range(2):
+                bank = psum.tile([P, 256, T], BF16, name="bank")
+                for j in range(2):
+                    c = 256 * i + 128 * j
+                    nc.tensor.matmul(bank[:, 128 * j : 128 * (j + 1), :], lhsT=ident_bf[:], rhs=src[:, :, c : c + 128].rearrange("p t c -> p c t"), start=True, stop=True)
+                banks.append(bank)
+            for i in range(2):
+                nc.scalar.copy(out=dst[:, 256 * i : 256 * (i + 1), :], in_=banks[i][:])
 
-        def quantize_x(b, g):
-            wide = stage.tile([P, T, S], BF16, name="wide")
-            for t in range(T):
-                nc.scalar.activation(out=wide[:, t, :], in_=xb[b, g][:, t * S : (t + 1) * S].bitcast(FP8), func=ACT.Copy, scale=xs[:, g, t : t + 1])
-            quads = stage.tile([P, S, T], BF16, name="quads", align_bytes=64)
-            nc.vector.tensor_copy(out=quads[:], in_=wide[:].rearrange("p t n -> p n t"))
+        def ile(b, g):
+            quads[b, g] = stage.tile([P, S, T], BF16, name="quads", align_bytes=64)
+            if (b, g) in PILED:
+                pile(wide[b, g], quads[b, g])
+            else:
+                nc.vector.tensor_copy(out=quads[b, g][:], in_=wide[b, g][:].rearrange("p t n -> p n t"))
+
+        def qnt(b, g):
             codes = keep.tile([P, S], U32, name="codes", align_bytes=64)
             scales = keep.tile([P, S], U8, name="scales", align_bytes=64)
-            nc.vector.quantize_mx(out=codes[:].bitcast(FP8X4), scales=scales[:], in_=quads[:].rearrange("p n t -> p (n t)"))
+            nc.vector.quantize_mx(out=codes[:].bitcast(FP8X4), scales=scales[:], in_=quads[b, g][:].rearrange("p n t -> p (n t)"))
             x_codes[b, g] = (codes, scales)
 
-        y = {}
-
-        def first_matmul(b, g):
+        def mm1(b, g):
             codes, scales = x_codes[b, g]
             for t in range(T):
                 if g == 0:
@@ -185,41 +213,57 @@ def tile_imagemla_pa_w4_kernel(tc, x_bytes, x_scale, q1_w_words, q1_w_scales, q1
                     stop=(g == G - 1),
                 )
 
-        h_codes = {}
+        def bn(b, t):
+            if t == 0:
+                stats[b] = {"st": small.tile([P, T, 2, 3], F32, name="st")}
+            nc.vector.bn_stats(out=stats[b]["st"][:, t].rearrange("p a b -> p (a b)"), in_=y[b, t][:])
 
-        def normalise(b):
-            st = small.tile([P, T, 2, 3], F32, name="st")
-            for t in range(T):
-                nc.vector.bn_stats(out=st[:, t].rearrange("p a b -> p (a b)"), in_=y[b, t][:])
+        def tot(b):
+            st = stats[b]["st"]
             nc.vector.tensor_tensor(out=st[:, :, :, 1], in0=st[:, :, :, 1], in1=gb[:, 0, :].unsqueeze(2).to_broadcast([P, T, 2]), op=ALU.add)
             ag = small.tile([P, 2], F32, name="ag")
             nc.vector.bn_aggr(out=ag[:], in_=st[:].rearrange("p t a b -> p (t a b)"))
             nc.vector.scalar_tensor_tensor(out=ag[:, 1:2], in0=ag[:, 0:1], scalar=ag[:, 0:1], in1=ag[:, 1:2], op0=ALU.mult, op1=ALU.add)
-            tot = psum.tile([P, S], F32, name="bank")
-            nc.tensor.matmul(tot[:, 0:2], lhsT=ones[:], rhs=ag[:], start=True, stop=True)
+            total = psum.tile([P, S], F32, name="bank")
+            nc.tensor.matmul(total[:, 0:2], lhsT=ones[:], rhs=ag[:], start=True, stop=True)
+            stats[b]["total"] = total
+
+        def rstd(b):
             mu = small.tile([P, 2], F32, name="mu")
-            nc.vector.tensor_copy(out=mu[:], in_=tot[:, 0:2])
+            nc.vector.tensor_copy(out=mu[:], in_=stats[b]["total"][:, 0:2])
             nvar = small.tile([P, 1], F32, name="nvar")
             nc.vector.scalar_tensor_tensor(out=nvar[:], in0=mu[:, 0:1], scalar=mu[:, 0:1], in1=mu[:, 1:2], op0=ALU.mult, op1=ALU.subtract)
-            nc.vector.tensor_scalar(out=nvar[:], in0=nvar[:], scalar1=-1.0, scalar2=EPS, op0=ALU.mult, op1=ALU.add)
-            rstd = small.tile([P, 1], F32, name="rstd")
-            nc.gpsimd.tensor_tensor(out=rstd[:], in0=nvar[:], in1=mhalf[:], op=ALU.pow)
+            vare = small.tile([P, 1], F32, name="vare")
+            nc.vector.tensor_scalar(out=vare[:], in0=nvar[:], scalar1=-1.0, scalar2=EPS, op0=ALU.mult, op1=ALU.add)
+            rs = small.tile([P, 1], F32, name="rs")
+            nc.gpsimd.tensor_tensor(out=rs[:], in0=vare[:], in1=mhalf[:], op=ALU.pow)
+            stats[b]["mu"] = mu
+            stats[b]["rs"] = rs
+
+        def aff(b):
             sc = small.tile([P, T], F32, name="sc")
-            nc.vector.tensor_scalar(out=sc[:], in0=gb[:, 1, :], scalar1=rstd[:], scalar2=None, op0=ALU.mult)
+            nc.vector.tensor_scalar(out=sc[:], in0=gb[:, 1, :], scalar1=stats[b]["rs"][:], scalar2=None, op0=ALU.mult)
             bi = small.tile([P, T], F32, name="bi")
-            nc.vector.scalar_tensor_tensor(out=bi[:], in0=gb[:, 0, :], scalar=mu[:, 0:1], in1=sc[:], op0=ALU.subtract, op1=ALU.mult)
-            nc.vector.tensor_tensor(out=bi[:], in0=bi[:], in1=gb[:, 2, :], op=ALU.add)
-            hw = stage.tile([P, T, S], BF16, name="hw", bufs=2)
-            for t in range(T):
-                nc.scalar.activation(out=hw[:, t, :], in_=y[b, t][:], func=ACT.Identity, scale=sc[:, t : t + 1], bias=bi[:, t : t + 1])
-            hq = stage.tile([P, S, T], BF16, name="hq", align_bytes=64, bufs=2)
-            nc.vector.tensor_copy(out=hq[:], in_=hw[:].rearrange("p t n -> p n t"))
+            nc.vector.scalar_tensor_tensor(out=bi[:], in0=gb[:, 0, :], scalar=stats[b]["mu"][:, 0:1], in1=sc[:], op0=ALU.subtract, op1=ALU.mult)
+            bj = small.tile([P, T], F32, name="bj")
+            nc.vector.tensor_tensor(out=bj[:], in0=bi[:], in1=gb[:, 2, :], op=ALU.add)
+            stats[b]["sc"] = sc
+            stats[b]["bi"] = bj
+
+        def nrm(b, t):
+            if t == 0:
+                hw[b] = stage.tile([P, T, S], BF16, name="hw", bufs=2)
+            nc.scalar.activation(out=hw[b][:, t, :], in_=y[b, t][:], func=ACT.Identity, scale=stats[b]["sc"][:, t : t + 1], bias=stats[b]["bi"][:, t : t + 1])
+
+        def hil(b):
+            hq[b] = stage.tile([P, S, T], BF16, name="hq", align_bytes=64, bufs=2)
+            nc.vector.tensor_copy(out=hq[b][:], in_=hw[b][:].rearrange("p t n -> p n t"))
+
+        def hqn(b):
             codes = keep.tile([P, S], U32, name="hcodes", align_bytes=64, bufs=2)
             scales = keep.tile([P, S], U8, name="hscales", align_bytes=64, bufs=2)
-            nc.vector.quantize_mx(out=codes[:].bitcast(FP8X4), scales=scales[:], in_=hq[:].rearrange("p n t -> p (n t)"))
+            nc.vector.quantize_mx(out=codes[:].bitcast(FP8X4), scales=scales[:], in_=hq[b][:].rearrange("p n t -> p (n t)"))
             h_codes[b] = (codes, scales)
-
-        b2 = const.tile([P, 2 * HEADS], F32, name="b2")
 
         def bias_columns():
             cols = psum.tile([P, S], F32, name="bank")
@@ -228,73 +272,211 @@ def tile_imagemla_pa_w4_kernel(tc, x_bytes, x_scale, q1_w_words, q1_w_scales, q1
                 nc.tensor.matmul(cols[:, i : i + 1], lhsT=qb[:, first : first + P], rhs=ones_bf[:, 0:1], start=True, stop=True)
             nc.vector.tensor_copy(out=b2[:], in_=cols[:, 0 : 2 * HEADS])
 
-        def head(b, h):
+        def zmm(b, h, dt):
             codes, scales = h_codes[b]
-            result = outs.tile([P, 4, HEAD_DIM], F32, name="result")
-            products = []
-            for dt in range(2):
-                first = HEAD_DIM * h + NOPE + P * dt
-                z = psum.tile([P, S], F32, name="bank")
+            first = HEAD_DIM * h + NOPE + P * dt
+            z[b, h, dt] = psum.tile([P, S], F32, name="bank")
+            nc.tensor.matmul_mx(
+                out=z[b, h, dt][:],
+                lhsT=w2[:, 2 * first : 2 * (first + P)].bitcast(FP4X4),
+                lhsT_scale=s2[:, first : first + P],
+                rhs=codes[:].bitcast(FP8X4),
+                rhs_scale=scales[:],
+                start=True,
+                stop=True,
+            )
+
+        def uu(b, h, dt):
+            u[b, h] = stage.tile([P, S], F32, name="u", bufs=3)
+            nc.scalar.activation(out=u[b, h][:], in_=z[b, h, dt][:], func=ACT.Identity, bias=b2[:, 2 * h + dt : 2 * h + dt + 1])
+
+        def gab(b, h, dt):
+            for k in range(2):
+                prod = stage.tile([P, S], F32, name="prod", bufs=12)
+                nc.gpsimd.tensor_tensor(out=prod[:], in0=u[b, h][:], in1=table[:, 2 * dt + k, :], op=ALU.mult)
+                prods[b, h, dt, k] = prod
+
+        def ab(b, h, dt):
+            for k in range(2):
+                prod = stage.tile([P, S], F32, name="prod", bufs=12)
+                nc.vector.scalar_tensor_tensor(out=prod[:], in0=z[b, h, dt][:], scalar=b2[:, 2 * h + dt : 2 * h + dt + 1], in1=table[:, 2 * dt + k, :], op0=ALU.add, op1=ALU.mult)
+                prods[b, h, dt, k] = prod
+
+        def result_half(b, h, half):
+            if (b, h) not in result:
+                result[b, h] = outs.tile([P, 4, HEAD_DIM], F32, name="result", bufs=4)
+            return result[b, h][:, 2 * half : 2 * half + 2]
+
+        def wrote(b, h, half):
+            if (b, h, half) in half_done:
+                nc.sync.dma_start(out=out[b, h].rearrange("(s p) d -> p s d", p=P)[:, 2 * half : 2 * half + 2], in_=result_half(b, h, half))
+            half_done.add((b, h, half))
+
+        def nmm(b, h, half):
+            codes, scales = h_codes[b]
+            bank = psum.tile([P, 2, NOPE], F32, name="bank")
+            for i in range(2):
+                st = 2 * half + i
                 nc.tensor.matmul_mx(
-                    out=z[:],
-                    lhsT=w2[:, 2 * first : 2 * (first + P)].bitcast(FP4X4),
-                    lhsT_scale=s2[:, first : first + P],
-                    rhs=codes[:].bitcast(FP8X4),
-                    rhs_scale=scales[:],
+                    out=bank[:, i, :],
+                    lhsT=codes[:, P * st : P * (st + 1)].bitcast(FP8X4),
+                    lhsT_scale=scales[:, P * st : P * (st + 1)],
+                    rhs=w2[:, 2 * HEAD_DIM * h : 2 * (HEAD_DIM * h + NOPE)].bitcast(FP4X4),
+                    rhs_scale=s2[:, HEAD_DIM * h : HEAD_DIM * h + NOPE],
                     start=True,
                     stop=True,
                 )
-                bias = b2[:, 2 * h + dt : 2 * h + dt + 1]
-                if dt == 1:
-                    u = stage.tile([P, S], F32, name="u", bufs=3)
-                    nc.scalar.activation(out=u[:], in_=z[:], func=ACT.Identity, bias=bias)
-                for k in range(2):
-                    prod = stage.tile([P, S], F32, name="prod", bufs=12)
-                    if dt == 1:
-                        nc.gpsimd.tensor_tensor(out=prod[:], in0=u[:], in1=table[:, 2 * dt + k, :], op=ALU.mult)
-                    else:
-                        nc.vector.scalar_tensor_tensor(out=prod[:], in0=z[:], scalar=bias, in1=table[:, 2 * dt + k, :], op0=ALU.add, op1=ALU.mult)
-                    products.append(prod)
-            for half in range(2):
-                n = psum.tile([P, S], F32, name="bank")
-                for i in range(2):
-                    st = 2 * half + i
-                    nc.tensor.matmul_mx(
-                        out=n[:, NOPE * i : NOPE * (i + 1)],
-                        lhsT=codes[:, P * st : P * (st + 1)].bitcast(FP8X4),
-                        lhsT_scale=scales[:, P * st : P * (st + 1)],
-                        rhs=w2[:, 2 * HEAD_DIM * h : 2 * (HEAD_DIM * h + NOPE)].bitcast(FP4X4),
-                        rhs_scale=s2[:, HEAD_DIM * h : HEAD_DIM * h + NOPE],
-                        start=True,
-                        stop=True,
-                    )
-                nc.vector.tensor_tensor(
-                    out=result[:, 2 * half : 2 * half + 2, 0:NOPE],
-                    in0=n[:].rearrange("p (i d) -> p i d", i=2),
-                    in1=qb[:, HEAD_DIM * h : HEAD_DIM * h + NOPE].unsqueeze(1).to_broadcast([P, 2, NOPE]),
-                    op=ALU.add,
-                )
-            for half in range(2):
-                o = psum.tile([P, S], F32, name="bank")
-                for i in range(2):
-                    st = 2 * half + i
-                    for dt in range(2):
-                        dst = o[:, NOPE * i + P * dt : NOPE * i + P * (dt + 1)]
-                        nc.tensor.matmul(dst, lhsT=products[2 * dt][:, P * st : P * (st + 1)], rhs=ident[:], is_transpose=True, start=True, stop=False)
-                        nc.tensor.matmul(dst, lhsT=products[2 * dt + 1][:, P * st : P * (st + 1)], rhs=swap[:], is_transpose=True, start=False, stop=True)
-                nc.scalar.copy(out=result[:, 2 * half : 2 * half + 2, NOPE:HEAD_DIM], in_=o[:].rearrange("p (i d) -> p i d", i=2))
-                nc.sync.dma_start(out=out[b, h].rearrange("(s p) d -> p s d", p=P)[:, 2 * half : 2 * half + 2], in_=result[:, 2 * half : 2 * half + 2])
+            n_bank[b, h, half] = bank
 
-        for g in range(G):
-            permute(g)
-            quantize_x(0, g)
-            first_matmul(0, g)
-        normalise(0)
-        for g in range(G):
-            quantize_x(1, g)
-            first_matmul(1, g)
-        normalise(1)
+        def nad(b, h, half):
+            nc.vector.tensor_tensor(
+                out=result_half(b, h, half)[:, :, 0:NOPE],
+                in0=n_bank[b, h, half][:],
+                in1=qb[:, HEAD_DIM * h : HEAD_DIM * h + NOPE].unsqueeze(1).to_broadcast([P, 2, NOPE]),
+                op=ALU.add,
+            )
+            wrote(b, h, half)
+
+        def nope1(b, h, half):
+            nmm(b, h, half)
+            nad(b, h, half)
+
+        def nope(b, h):
+            for half in range(2):
+                nope1(b, h, half)
+
+        def tail1(b, h, half):
+            bank = psum.tile([P, 2, NOPE], F32, name="bank")
+            for i in range(2):
+                st = 2 * half + i
+                for dt in range(2):
+                    dst = bank[:, i, P * dt : P * (dt + 1)]
+                    nc.tensor.matmul(dst, lhsT=prods[b, h, dt, 0][:, P * st : P * (st + 1)], rhs=ident[:], is_transpose=True, start=True, stop=False)
+                    nc.tensor.matmul(dst, lhsT=prods[b, h, dt, 1][:, P * st : P * (st + 1)], rhs=swap[:], is_transpose=True, start=False, stop=True)
+            nc.scalar.copy(out=result_half(b, h, half)[:, :, NOPE:HEAD_DIM], in_=bank[:])
+            wrote(b, h, half)
+
+        def tail(b, h):
+            for half in range(2):
+                tail1(b, h, half)
+
+        for t in range(2):
+            widen(0, 0, t)
+        for t in range(2, T):
+            widen(0, 0, t, on_vector=True)
+        for t in range(T):
+            widen(0, 1, t)
+        angles()
+        sines()
+        ile(0, 0)
+        for g in range(2, G):
+            for t in range(T):
+                widen(0, g, t)
+        perm(0)
+        perm(1)
+        perm(2)
+        ile(0, 1)
+        perm(3)
+        qnt(0, 0)
+        mm1(0, 0)
+        ile(0, 2)
+        qnt(0, 1)
+        mm1(0, 1)
+        qnt(0, 2)
+        mm1(0, 2)
+        ile(0, 3)
+        qnt(0, 3)
+        mm1(0, 3)
+        ahead = [(g, t) for g in range(G) for t in range(T)]
+        for g, t in ahead[:14]:
+            widen(1, g, t)
+        tabx(0)
+        for t in range(T):
+            bn(0, t)
+        tot(0)
+        tabx(1)
+        rstd(0)
+        ile(1, 1)
+        aff(0)
+        for t in range(T):
+            nrm(0, t)
+        ile(1, 0)
+        tabx(2)
+        qnt(1, 0)
+        mm1(1, 0)
         bias_columns()
-        for b in range(B):
-            for h in range(HEADS):
-                head(b, h)
+        hil(0)
+        tabx(3)
+        hqn(0)
+        for g, t in ahead[14:]:
+            widen(1, g, t)
+        zmm(0, 0, 1)
+        uu(0, 0, 1)
+        gab(0, 0, 1)
+        zmm(0, 0, 0)
+        ile(1, 2)
+        qnt(1, 1)
+        ab(0, 0, 0)
+        ile(1, 3)
+        qnt(1, 2)
+        mm1(1, 1)
+        nope1(0, 0, 0)
+        qnt(1, 3)
+        zmm(0, 1, 0)
+        mm1(1, 2)
+        mm1(1, 3)
+        ab(0, 1, 0)
+        zmm(0, 1, 1)
+        uu(0, 1, 1)
+        gab(0, 1, 1)
+        tail1(0, 0, 0)
+        tail1(0, 0, 1)
+        nmm(0, 0, 1)
+        for t in range(T):
+            bn(1, t)
+        zmm(0, 2, 1)
+        tot(1)
+        uu(0, 2, 1)
+        nad(0, 0, 1)
+        nmm(0, 1, 0)
+        rstd(1)
+        gab(0, 2, 1)
+        nad(0, 1, 0)
+        aff(1)
+        for t in range(T):
+            nrm(1, t)
+        zmm(0, 2, 0)
+        nmm(0, 1, 1)
+        tail1(0, 1, 0)
+        tail1(0, 1, 1)
+        ab(0, 2, 0)
+        nad(0, 1, 1)
+        zmm(0, 3, 1)
+        uu(0, 3, 1)
+        gab(0, 3, 1)
+        nmm(0, 2, 0)
+        hil(1)
+        nad(0, 2, 0)
+        hqn(1)
+        zmm(0, 3, 0)
+        ab(0, 3, 0)
+        nmm(0, 2, 1)
+        nad(0, 2, 1)
+        tail1(0, 2, 0)
+        tail1(0, 2, 1)
+        zmm(1, 0, 1)
+        uu(1, 0, 1)
+        gab(1, 0, 1)
+        last = (0, 3)
+        for h in range(HEADS):
+            zmm(1, h, 0)
+            ab(1, h, 0)
+            if h < 3:
+                zmm(1, h + 1, 1)
+                uu(1, h + 1, 1)
+                gab(1, h + 1, 1)
+            nope(*last)
+            tail(*last)
+            last = (1, h)
+        nope(*last)
+        tail(*last)

@@ -43,8 +43,14 @@ def tile_imagemla_pa_w4_kernel(tc, x_bytes, x_scale, q1_w_words, q1_w_scales, q1
         nc.vector.memset(dummy[:], 0.0)
         nc.scalar.activation(out=dummy[:], in_=dummy[:], func=ACT.Sin)
 
-        xs = const.tile([P, G, T], F32, name="xs")
-        nc.sync.dma_start(out=xs[:], in_=x_scale.rearrange("a (g p t) c d -> p (a g) (t c d)", p=P, t=T))
+        xs = {}
+
+        def load_scale(g):
+            tile = const.tile([P, T], F32, name="xs%d" % g)
+            nc.sync.dma_start(out=tile[:], in_=x_scale.rearrange("a (g p t) c d -> p (a g) (t c d)", p=P, t=T)[:, g])
+            xs[g] = tile
+
+        load_scale(0)
         x_rows = x_bytes.rearrange("b (g p t) h w -> b g p (t h w)", p=P, t=T)
         xb = {}
 
@@ -54,8 +60,6 @@ def tile_imagemla_pa_w4_kernel(tc, x_bytes, x_scale, q1_w_words, q1_w_scales, q1
             xb[b, g] = tile
 
         load_x(0, 0)
-        w1_raw = const.tile([P, G, 2 * Q_RANK], U8, name="w1_raw", align_bytes=64)
-        nc.sync.dma_start(out=w1_raw[:], in_=q1_w_words.rearrange("g p n -> p g n"))
         s1_raw = const.tile([P, G, Q_RANK], U8, name="s1_raw", align_bytes=64)
         nc.vector.memset(s1_raw[:].rearrange("p g n -> p (g n)").bitcast(I32), 0)
         s2 = const.tile([P, HEADS * HEAD_DIM], U8, name="s2", align_bytes=64)
@@ -63,7 +67,10 @@ def tile_imagemla_pa_w4_kernel(tc, x_bytes, x_scale, q1_w_words, q1_w_scales, q1
         s1_view = s1_raw[:].rearrange("p g n -> p (g n)").bitcast(I32).rearrange("p (g n) -> p g n", g=G)
         for q in range(4):
             nc.sync.dma_start(out=s1_view[32 * q : 32 * q + 4], in_=q1_w_scales.bitcast(I32)[:, 4 * q : 4 * q + 4, :].rearrange("g r n -> r g n"))
+        w1_raw = const.tile([P, G, 2 * Q_RANK], U8, name="w1_raw", align_bytes=64)
+        nc.sync.dma_start(out=w1_raw[:], in_=q1_w_words.rearrange("g p n -> p g n"))
         for g in range(1, G):
+            load_scale(g)
             load_x(0, g)
         vecs = {}
         for name, ap in (("q1_b", q1_b), ("q_gn_g", q_gn_g), ("q_gn_b", q_gn_b)):
@@ -170,9 +177,9 @@ def tile_imagemla_pa_w4_kernel(tc, x_bytes, x_scale, q1_w_words, q1_w_scales, q1
                 wide[b, g] = stage.tile([P, T, S], BF16, name="wide", bufs=8)
             src = xb[b, g][:, t * S : (t + 1) * S].bitcast(FP8)
             if on_vector:
-                nc.vector.tensor_scalar(out=wide[b, g][:, t, :], in0=src, scalar1=xs[:, g, t : t + 1], scalar2=None, op0=ALU.mult)
+                nc.vector.tensor_scalar(out=wide[b, g][:, t, :], in0=src, scalar1=xs[g][:, t : t + 1], scalar2=None, op0=ALU.mult)
             else:
-                nc.scalar.activation(out=wide[b, g][:, t, :], in_=src, func=ACT.Copy, scale=xs[:, g, t : t + 1])
+                nc.scalar.activation(out=wide[b, g][:, t, :], in_=src, func=ACT.Copy, scale=xs[g][:, t : t + 1])
 
         def pile(src, dst):
             banks = []
@@ -229,22 +236,20 @@ def tile_imagemla_pa_w4_kernel(tc, x_bytes, x_scale, q1_w_words, q1_w_scales, q1
             stats[b]["total"] = total
 
         def rstd(b):
-            mu = small.tile([P, 2], F32, name="mu")
-            nc.vector.tensor_copy(out=mu[:], in_=stats[b]["total"][:, 0:2])
-            nvar = small.tile([P, 1], F32, name="nvar")
-            nc.vector.scalar_tensor_tensor(out=nvar[:], in0=mu[:, 0:1], scalar=mu[:, 0:1], in1=mu[:, 1:2], op0=ALU.mult, op1=ALU.subtract)
+            total = stats[b]["total"]
+            mu2 = small.tile([P, 1], F32, name="mu2")
+            nc.vector.tensor_scalar(out=mu2[:], in0=total[:, 0:1], scalar1=total[:, 0:1], scalar2=None, op0=ALU.mult)
             vare = small.tile([P, 1], F32, name="vare")
-            nc.vector.tensor_scalar(out=vare[:], in0=nvar[:], scalar1=-1.0, scalar2=EPS, op0=ALU.mult, op1=ALU.add)
+            nc.vector.tensor_scalar(out=vare[:], in0=total[:, 1:2], scalar1=mu2[:], scalar2=EPS, op0=ALU.subtract, op1=ALU.add)
             rs = small.tile([P, 1], F32, name="rs")
             nc.gpsimd.tensor_tensor(out=rs[:], in0=vare[:], in1=mhalf[:], op=ALU.pow)
-            stats[b]["mu"] = mu
             stats[b]["rs"] = rs
 
         def aff(b):
             sc = small.tile([P, T], F32, name="sc")
             nc.vector.tensor_scalar(out=sc[:], in0=gb[:, 1, :], scalar1=stats[b]["rs"][:], scalar2=None, op0=ALU.mult)
             bi = small.tile([P, T], F32, name="bi")
-            nc.vector.scalar_tensor_tensor(out=bi[:], in0=gb[:, 0, :], scalar=stats[b]["mu"][:, 0:1], in1=sc[:], op0=ALU.subtract, op1=ALU.mult)
+            nc.vector.scalar_tensor_tensor(out=bi[:], in0=gb[:, 0, :], scalar=stats[b]["total"][:, 0:1], in1=sc[:], op0=ALU.subtract, op1=ALU.mult)
             bj = small.tile([P, T], F32, name="bj")
             nc.vector.tensor_tensor(out=bj[:], in0=bi[:], in1=gb[:, 2, :], op=ALU.add)
             stats[b]["sc"] = sc
@@ -356,35 +361,47 @@ def tile_imagemla_pa_w4_kernel(tc, x_bytes, x_scale, q1_w_words, q1_w_scales, q1
             nc.scalar.copy(out=result_half(b, h, half)[:, :, NOPE:HEAD_DIM], in_=bank[:])
             wrote(b, h, half)
 
+        def last_tail(b, h):
+            for st in range(4):
+                bank = psum.tile([P, NOPE], F32, name="bank")
+                for dt in range(2):
+                    dst = bank[:, P * dt : P * (dt + 1)]
+                    nc.tensor.matmul(dst, lhsT=prods[b, h, dt, 0][:, P * st : P * (st + 1)], rhs=ident[:], is_transpose=True, start=True, stop=False)
+                    nc.tensor.matmul(dst, lhsT=prods[b, h, dt, 1][:, P * st : P * (st + 1)], rhs=swap[:], is_transpose=True, start=False, stop=True)
+                piece = result[b, h][:, st]
+                if st % 2 == 0:
+                    nc.scalar.copy(out=piece[:, NOPE:HEAD_DIM], in_=bank[:])
+                else:
+                    nc.vector.tensor_copy(out=piece[:, NOPE:HEAD_DIM], in_=bank[:])
+                nc.sync.dma_start(out=out[b, h].rearrange("(s p) d -> p s d", p=P)[:, st], in_=piece)
+
         def tail(b, h):
             for half in range(2):
                 tail1(b, h, half)
 
+        angles()
         for t in range(2):
             widen(0, 0, t)
         for t in range(2, T):
             widen(0, 0, t, on_vector=True)
-        for t in range(T):
-            widen(0, 1, t)
-        angles()
-        sines()
-        ile(0, 0)
-        for g in range(2, G):
+        for g in range(1, G):
             for t in range(T):
                 widen(0, g, t)
+        sines()
+        ile(0, 0)
         perm(0)
-        perm(1)
-        perm(2)
-        ile(0, 1)
-        perm(3)
         qnt(0, 0)
         mm1(0, 0)
+        perm(1)
+        ile(0, 1)
+        perm(2)
         ile(0, 2)
         qnt(0, 1)
         mm1(0, 1)
         qnt(0, 2)
         mm1(0, 2)
         ile(0, 3)
+        perm(3)
         qnt(0, 3)
         mm1(0, 3)
         ahead = [(g, t) for g in range(G) for t in range(T)]
@@ -393,80 +410,74 @@ def tile_imagemla_pa_w4_kernel(tc, x_bytes, x_scale, q1_w_words, q1_w_scales, q1
         tabx(0)
         for t in range(T):
             bn(0, t)
-        tot(0)
         tabx(1)
+        tot(0)
+        ile(1, 0)
         rstd(0)
         ile(1, 1)
+        for g, t in ahead[14:]:
+            widen(1, g, t)
+        qnt(1, 0)
         aff(0)
         for t in range(T):
             nrm(0, t)
-        ile(1, 0)
-        tabx(2)
-        qnt(1, 0)
-        mm1(1, 0)
-        bias_columns()
-        hil(0)
-        tabx(3)
-        hqn(0)
-        for g, t in ahead[14:]:
-            widen(1, g, t)
-        zmm(0, 0, 1)
-        uu(0, 0, 1)
-        gab(0, 0, 1)
-        zmm(0, 0, 0)
         ile(1, 2)
         qnt(1, 1)
-        ab(0, 0, 0)
-        ile(1, 3)
-        qnt(1, 2)
+        mm1(1, 0)
         mm1(1, 1)
-        nope1(0, 0, 0)
+        ile(1, 3)
+        tabx(2)
+        bias_columns()
+        hil(0)
+        qnt(1, 2)
+        hqn(0)
+        tabx(3)
         qnt(1, 3)
-        zmm(0, 1, 0)
+        zmm(0, 0, 0)
+        zmm(0, 0, 1)
         mm1(1, 2)
         mm1(1, 3)
-        ab(0, 1, 0)
+        uu(0, 0, 1)
+        ab(0, 0, 0)
+        nmm(0, 0, 0)
         zmm(0, 1, 1)
-        uu(0, 1, 1)
-        gab(0, 1, 1)
-        tail1(0, 0, 0)
-        tail1(0, 0, 1)
         nmm(0, 0, 1)
         for t in range(T):
             bn(1, t)
-        zmm(0, 2, 1)
+        uu(0, 1, 1)
         tot(1)
-        uu(0, 2, 1)
-        nad(0, 0, 1)
-        nmm(0, 1, 0)
+        gab(0, 0, 1)
         rstd(1)
-        gab(0, 2, 1)
-        nad(0, 1, 0)
+        nad(0, 0, 0)
         aff(1)
         for t in range(T):
             nrm(1, t)
+        nad(0, 0, 1)
+        zmm(0, 1, 0)
+        nmm(0, 1, 0)
+        tail(0, 0)
+        ab(0, 1, 0)
+        gab(0, 1, 1)
+        nad(0, 1, 0)
+        hil(1)
+        hqn(1)
+        zmm(0, 2, 1)
+        uu(0, 2, 1)
+        gab(0, 2, 1)
+        nope1(0, 1, 1)
         zmm(0, 2, 0)
-        nmm(0, 1, 1)
-        tail1(0, 1, 0)
-        tail1(0, 1, 1)
         ab(0, 2, 0)
-        nad(0, 1, 1)
+        tail(0, 1)
         zmm(0, 3, 1)
         uu(0, 3, 1)
         gab(0, 3, 1)
-        nmm(0, 2, 0)
-        hil(1)
-        nad(0, 2, 0)
-        hqn(1)
+        nope(0, 2)
         zmm(0, 3, 0)
         ab(0, 3, 0)
-        nmm(0, 2, 1)
-        nad(0, 2, 1)
-        tail1(0, 2, 0)
-        tail1(0, 2, 1)
         zmm(1, 0, 1)
         uu(1, 0, 1)
         gab(1, 0, 1)
+        tail(0, 2)
         last = (0, 3)
         for h in range(HEADS):
             zmm(1, h, 0)
@@ -476,7 +487,8 @@ def tile_imagemla_pa_w4_kernel(tc, x_bytes, x_scale, q1_w_words, q1_w_scales, q1
                 uu(1, h + 1, 1)
                 gab(1, h + 1, 1)
             nope(*last)
+            if h == HEADS - 1:
+                nope(1, h)
             tail(*last)
             last = (1, h)
-        nope(*last)
-        tail(*last)
+        last_tail(*last)

@@ -153,18 +153,22 @@ def tile_imagemla_pa_w4_kernel(tc, x_bytes, x_scale, q1_w_words, q1_w_scales, q1
             nc.vector.tensor_copy(out=whole[:], in_=turns_flat)
             nc.vector.tensor_tensor(out=frac[:], in0=turns_flat, in1=whole[:], op=ALU.subtract)
             nc.vector.scalar_tensor_tensor(out=wrapped[:].rearrange("p d k n -> p (d k n)"), in0=frac[:], scalar=0.5, in1=frac[:], op0=ALU.is_gt, op1=ALU.subtract)
-            for k in range(2):
-                for axis, cols in ((0, slice(0, H)), (1, slice(H, H + W))):
-                    nc.vector.tensor_scalar(out=masked[:, :, k, cols], in0=wrapped[:, :, k, cols], scalar1=factor[:, k, axis : axis + 1], scalar2=None, op0=ALU.mult)
+            for axis, cols in ((0, slice(0, H)), (1, slice(H, H + W))):
+                nc.vector.tensor_tensor(
+                    out=masked[:, :, :, cols],
+                    in0=wrapped[:, :, :, cols],
+                    in1=factor[:, :, axis].unsqueeze(1).unsqueeze(3).to_broadcast([P, 2, 2, cols.stop - cols.start]),
+                    op=ALU.mult,
+                )
 
         def sines():
             nc.scalar.activation(out=waves[:].rearrange("p k n -> p (k n)"), in_=masked[:].rearrange("p d k n -> p (d k n)"), func=ACT.Sin, scale=-2 * math.pi)
 
-        def tabx(k):
+        def tabx(dt):
             nc.vector.tensor_tensor(
-                out=table[:, k, :].rearrange("p (h w) -> p h w", h=H),
-                in0=waves[:, k, 0:H].unsqueeze(2).to_broadcast([P, H, W]),
-                in1=waves[:, k, H : H + W].unsqueeze(1).to_broadcast([P, H, W]),
+                out=table[:, 2 * dt : 2 * dt + 2, :].rearrange("p k (h w) -> p k h w", h=H),
+                in0=waves[:, 2 * dt : 2 * dt + 2, 0:H].unsqueeze(3).to_broadcast([P, 2, H, W]),
+                in1=waves[:, 2 * dt : 2 * dt + 2, H : H + W].unsqueeze(2).to_broadcast([P, 2, H, W]),
                 op=ALU.add,
             )
 
@@ -197,7 +201,7 @@ def tile_imagemla_pa_w4_kernel(tc, x_bytes, x_scale, q1_w_words, q1_w_scales, q1
             if (b, g) in PILED:
                 pile(wide[b, g], quads[b, g])
             else:
-                nc.vector.tensor_copy(out=quads[b, g][:], in_=wide[b, g][:].rearrange("p t n -> p n t"))
+                nc.vector.tensor_copy(out=quads[b, g][:].rearrange("p (c i) t -> p c t i", i=4), in_=wide[b, g][:].rearrange("p t (c i) -> p c t i", i=4))
 
         def qnt(b, g):
             codes = keep.tile([P, S], U32, name="codes", align_bytes=64)
@@ -262,7 +266,7 @@ def tile_imagemla_pa_w4_kernel(tc, x_bytes, x_scale, q1_w_words, q1_w_scales, q1
 
         def hil(b):
             hq[b] = stage.tile([P, S, T], BF16, name="hq", align_bytes=64, bufs=2)
-            nc.vector.tensor_copy(out=hq[b][:], in_=hw[b][:].rearrange("p t n -> p n t"))
+            nc.vector.tensor_copy(out=hq[b][:].rearrange("p (c i) t -> p c t i", i=4), in_=hw[b][:].rearrange("p t (c i) -> p c t i", i=4))
 
         def hqn(b):
             codes = keep.tile([P, S], U32, name="hcodes", align_bytes=64, bufs=2)
@@ -296,16 +300,21 @@ def tile_imagemla_pa_w4_kernel(tc, x_bytes, x_scale, q1_w_words, q1_w_scales, q1
             nc.scalar.activation(out=u[b, h][:], in_=z[b, h, dt][:], func=ACT.Identity, bias=b2[:, 2 * h + dt : 2 * h + dt + 1])
 
         def gab(b, h, dt):
-            for k in range(2):
-                prod = stage.tile([P, S], F32, name="prod", bufs=12)
-                nc.gpsimd.tensor_tensor(out=prod[:], in0=u[b, h][:], in1=table[:, 2 * dt + k, :], op=ALU.mult)
-                prods[b, h, dt, k] = prod
+            prod = stage.tile([P, 2, S], F32, name="prod", bufs=6)
+            nc.gpsimd.tensor_tensor(out=prod[:], in0=u[b, h][:].unsqueeze(1).to_broadcast([P, 2, S]), in1=table[:, 2 * dt : 2 * dt + 2, :], op=ALU.mult)
+            prods[b, h, dt] = prod
 
         def ab(b, h, dt):
-            for k in range(2):
-                prod = stage.tile([P, S], F32, name="prod", bufs=12)
-                nc.vector.scalar_tensor_tensor(out=prod[:], in0=z[b, h, dt][:], scalar=b2[:, 2 * h + dt : 2 * h + dt + 1], in1=table[:, 2 * dt + k, :], op0=ALU.add, op1=ALU.mult)
-                prods[b, h, dt, k] = prod
+            prod = stage.tile([P, 2, S], F32, name="prod", bufs=6)
+            nc.vector.scalar_tensor_tensor(
+                out=prod[:],
+                in0=z[b, h, dt][:].unsqueeze(1).to_broadcast([P, 2, S]),
+                scalar=b2[:, 2 * h + dt : 2 * h + dt + 1],
+                in1=table[:, 2 * dt : 2 * dt + 2, :],
+                op0=ALU.add,
+                op1=ALU.mult,
+            )
+            prods[b, h, dt] = prod
 
         def result_half(b, h, half):
             if (b, h) not in result:
@@ -356,8 +365,8 @@ def tile_imagemla_pa_w4_kernel(tc, x_bytes, x_scale, q1_w_words, q1_w_scales, q1
                 st = 2 * half + i
                 for dt in range(2):
                     dst = bank[:, i, P * dt : P * (dt + 1)]
-                    nc.tensor.matmul(dst, lhsT=prods[b, h, dt, 0][:, P * st : P * (st + 1)], rhs=ident[:], is_transpose=True, start=True, stop=False)
-                    nc.tensor.matmul(dst, lhsT=prods[b, h, dt, 1][:, P * st : P * (st + 1)], rhs=swap[:], is_transpose=True, start=False, stop=True)
+                    nc.tensor.matmul(dst, lhsT=prods[b, h, dt][:, 0, P * st : P * (st + 1)], rhs=ident[:], is_transpose=True, start=True, stop=False)
+                    nc.tensor.matmul(dst, lhsT=prods[b, h, dt][:, 1, P * st : P * (st + 1)], rhs=swap[:], is_transpose=True, start=False, stop=True)
             nc.scalar.copy(out=result_half(b, h, half)[:, :, NOPE:HEAD_DIM], in_=bank[:])
             wrote(b, h, half)
 
@@ -366,8 +375,8 @@ def tile_imagemla_pa_w4_kernel(tc, x_bytes, x_scale, q1_w_words, q1_w_scales, q1
                 bank = psum.tile([P, NOPE], F32, name="bank")
                 for dt in range(2):
                     dst = bank[:, P * dt : P * (dt + 1)]
-                    nc.tensor.matmul(dst, lhsT=prods[b, h, dt, 0][:, P * st : P * (st + 1)], rhs=ident[:], is_transpose=True, start=True, stop=False)
-                    nc.tensor.matmul(dst, lhsT=prods[b, h, dt, 1][:, P * st : P * (st + 1)], rhs=swap[:], is_transpose=True, start=False, stop=True)
+                    nc.tensor.matmul(dst, lhsT=prods[b, h, dt][:, 0, P * st : P * (st + 1)], rhs=ident[:], is_transpose=True, start=True, stop=False)
+                    nc.tensor.matmul(dst, lhsT=prods[b, h, dt][:, 1, P * st : P * (st + 1)], rhs=swap[:], is_transpose=True, start=False, stop=True)
                 piece = result[b, h][:, st]
                 if st % 2 == 0:
                     nc.scalar.copy(out=piece[:, NOPE:HEAD_DIM], in_=bank[:])
@@ -407,13 +416,12 @@ def tile_imagemla_pa_w4_kernel(tc, x_bytes, x_scale, q1_w_words, q1_w_scales, q1
         ahead = [(g, t) for g in range(G) for t in range(T)]
         for g, t in ahead[:14]:
             widen(1, g, t)
-        tabx(0)
         for t in range(T):
             bn(0, t)
-        tabx(1)
         tot(0)
         ile(1, 0)
         rstd(0)
+        tabx(0)
         ile(1, 1)
         for g, t in ahead[14:]:
             widen(1, g, t)
@@ -426,12 +434,11 @@ def tile_imagemla_pa_w4_kernel(tc, x_bytes, x_scale, q1_w_words, q1_w_scales, q1
         mm1(1, 0)
         mm1(1, 1)
         ile(1, 3)
-        tabx(2)
         bias_columns()
         hil(0)
         qnt(1, 2)
         hqn(0)
-        tabx(3)
+        tabx(1)
         qnt(1, 3)
         zmm(0, 0, 0)
         zmm(0, 0, 1)
@@ -477,15 +484,16 @@ def tile_imagemla_pa_w4_kernel(tc, x_bytes, x_scale, q1_w_words, q1_w_scales, q1
         zmm(1, 0, 1)
         uu(1, 0, 1)
         gab(1, 0, 1)
+        zmm(1, 0, 0)
         tail(0, 2)
         last = (0, 3)
         for h in range(HEADS):
-            zmm(1, h, 0)
             ab(1, h, 0)
             if h < 3:
                 zmm(1, h + 1, 1)
                 uu(1, h + 1, 1)
                 gab(1, h + 1, 1)
+                zmm(1, h + 1, 0)
             nope(*last)
             if h == HEADS - 1:
                 nope(1, h)

import math
from contextlib import ExitStack

import concourse.mybir as mybir
from concourse.masks import make_identity

F32 = mybir.dt.float32
BF16 = mybir.dt.bfloat16
I32 = mybir.dt.int32
U32 = mybir.dt.uint32
U8 = mybir.dt.uint8
FP8 = mybir.dt.float8_e4m3fn
FP8X4 = mybir.dt.float8_e4m3fn_x4
FP4X4 = mybir.dt.float4_e2m1fn_x4
ALU = mybir.AluOpType
ACT = mybir.ActivationFunctionType

P = 128
B, H, W, DIM, HEADS, Q_RANK = 2, 32, 16, 2048, 4, 512
S = H * W
HEAD_DIM = 512
NOPE = 256
G = DIM // 512
T = 4
EPS = 1e-5
PILED = {(1, 1), (1, 3)}
FLOPS = 2 * B * S * (DIM * Q_RANK + Q_RANK * HEADS * HEAD_DIM)


def tile_imagemla_pa_w4_kernel(tc, x_bytes, x_scale, q1_w_words, q1_w_scales, q1_b, q_gn_g, q_gn_b, q2_w_words, q2_w_scales, q2_b, out):
    nc = tc.nc
    with ExitStack() as ctx:
        const = ctx.enter_context(tc.tile_pool(name="const", bufs=1))
        small = ctx.enter_context(tc.tile_pool(name="small", bufs=2))
        xin = ctx.enter_context(tc.tile_pool(name="xin", bufs=8))
        stage = ctx.enter_context(tc.tile_pool(name="stage", bufs=4))
        keep = ctx.enter_context(tc.tile_pool(name="keep", bufs=8))
        outs = ctx.enter_context(tc.tile_pool(name="outs", bufs=3))
        psum = ctx.enter_context(tc.psum_pool(name="psum", bufs=8))

        ctx.enter_context(tc.manual_schedule())
        dummy = const.tile([P, 1], F32, name="dummy")
        nc.vector.memset(dummy[:], 0.0)
        nc.scalar.activation(out=dummy[:], in_=dummy[:], func=ACT.Sin)

        xs = {}

        def load_scale(g):
            tile = const.tile([P, T], F32, name="xs%d" % g)
            nc.sync.dma_start(out=tile[:], in_=x_scale.rearrange("a (g p t) c d -> p (a g) (t c d)", p=P, t=T)[:, g])
            xs[g] = tile

        load_scale(0)
        x_rows = x_bytes.rearrange("b (g p t) h w -> b g p (t h w)", p=P, t=T)
        xb = {}

        def load_x(b, g):
            tile = xin.tile([P, T * S], U8, name="xb")
            nc.sync.dma_start(out=tile[:], in_=x_rows[b, g])
            xb[b, g] = tile

        load_x(0, 0)
        s1_raw = const.tile([P, G, Q_RANK], U8, name="s1_raw", align_bytes=64)
        nc.vector.memset(s1_raw[:].rearrange("p g n -> p (g n)").bitcast(I32), 0)
        s2 = const.tile([P, HEADS * HEAD_DIM], U8, name="s2", align_bytes=64)
        nc.vector.memset(s2[:].bitcast(I32), 0)
        s1_view = s1_raw[:].rearrange("p g n -> p (g n)").bitcast(I32).rearrange("p (g n) -> p g n", g=G)
        for q in range(4):
            nc.sync.dma_start(out=s1_view[32 * q : 32 * q + 4], in_=q1_w_scales.bitcast(I32)[:, 4 * q : 4 * q + 4, :].rearrange("g r n -> r g n"))
        w1_raw = const.tile([P, G, 2 * Q_RANK], U8, name="w1_raw", align_bytes=64)
        nc.sync.dma_start(out=w1_raw[:], in_=q1_w_words.rearrange("g p n -> p g n"))
        for g in range(1, G):
            load_scale(g)
            load_x(0, g)
        vecs = {}
        for name, ap in (("q1_b", q1_b), ("q_gn_g", q_gn_g), ("q_gn_b", q_gn_b)):
            v = const.tile([P, T], BF16, name="v_" + name)
            nc.sync.dma_start(out=v[:], in_=ap.rearrange("(p t) -> p t", t=T))
            vecs[name] = v
        for g in range(G):
            load_x(1, g)
        w2 = const.tile([P, 2 * HEADS * HEAD_DIM], U8, name="w2", align_bytes=64)
        nc.sync.dma_start(out=w2[:], in_=q2_w_words[0])
        for q in range(4):
            nc.sync.dma_start(out=s2[32 * q : 32 * q + 4, :].bitcast(I32), in_=q2_w_scales.bitcast(I32)[0, 4 * q : 4 * q + 4, :])
        qb = const.tile([P, HEADS * HEAD_DIM], BF16, name="qb")
        nc.sync.dma_start(out=qb[:], in_=q2_b.partition_broadcast(P))


        part = const.tile([P, 1], I32, name="part")
        nc.gpsimd.iota(part[:], pattern=[[0, 1]], base=0, channel_multiplier=1)
        first_m = const.tile([P, 2], F32, name="first_m")
        nc.gpsimd.iota(first_m[:], pattern=[[32, 2]], base=0, channel_multiplier=0, allow_small_or_imprecise_dtypes=True)
        base = const.tile([P, 2], F32, name="base")
        nc.gpsimd.memset(base[:], 10000.0)
        pos = const.tile([P, H + W], F32, name="pos")
        nc.gpsimd.iota(pos[:, 0:H], pattern=[[1, H]], base=0, channel_multiplier=0, allow_small_or_imprecise_dtypes=True)
        nc.gpsimd.iota(pos[:, H : H + W], pattern=[[1, W]], base=0, channel_multiplier=0, allow_small_or_imprecise_dtypes=True)
        bits_i = const.tile([P, 3], I32, name="bits_i")
        nc.vector.tensor_scalar(out=bits_i[:, 0:1], in0=part[:], scalar1=2, scalar2=None, op0=ALU.arith_shift_right)
        nc.vector.tensor_scalar(out=bits_i[:, 1:2], in0=part[:], scalar1=1, scalar2=1, op0=ALU.arith_shift_right, op1=ALU.bitwise_and)
        nc.vector.tensor_scalar(out=bits_i[:, 2:3], in0=part[:], scalar1=1, scalar2=None, op0=ALU.bitwise_and)
        bits = const.tile([P, 3], F32, name="bits")
        nc.vector.tensor_copy(out=bits[:], in_=bits_i[:])
        expo = const.tile([P, 2], F32, name="expo")
        nc.vector.tensor_scalar(out=expo[:], in0=first_m[:], scalar1=bits[:, 0:1], scalar2=-1.0 / 64, op0=ALU.add, op1=ALU.mult)
        inv = const.tile([P, 2], F32, name="inv")
        nc.gpsimd.tensor_tensor(out=inv[:], in0=base[:], in1=expo[:], op=ALU.pow)
        factor = const.tile([P, 2, 2], F32, name="factor")
        sign = const.tile([P, 1], F32, name="sign")
        nc.vector.tensor_scalar(out=factor[:, 0, 0:1], in0=bits[:, 1:2], scalar1=-1.0, scalar2=1.0, op0=ALU.mult, op1=ALU.add)
        nc.vector.tensor_scalar(out=sign[:], in0=bits[:, 2:3], scalar1=-2.0, scalar2=1.0, op0=ALU.mult, op1=ALU.add)
        nc.vector.tensor_copy(out=factor[:, 0, 1:2], in_=bits[:, 1:2])
        nc.vector.tensor_scalar(out=factor[:, 1, :], in0=factor[:, 0, :], scalar1=sign[:], scalar2=None, op0=ALU.mult)
        turns = const.tile([P, 2, 2, H + W], F32, name="turns")
        whole = const.tile([P, 4 * (H + W)], I32, name="whole")
        frac = const.tile([P, 4 * (H + W)], F32, name="frac")
        wrapped = const.tile([P, 2, 2, H + W], F32, name="wrapped")
        masked = const.tile([P, 2, 2, H + W], F32, name="masked")
        waves = const.tile([P, 4, H + W], F32, name="waves")
        table = const.tile([P, 4, S], F32, name="table")

        ident = const.tile([P, P], F32, name="ident")
        make_identity(nc, ident[:])
        ones = const.tile([P, P], F32, name="ones")
        nc.gpsimd.memset(ones[:], 1.0 / P)
        ones_bf = const.tile([P, 2], BF16, name="ones_bf")
        nc.gpsimd.memset(ones_bf[:], 1.0 / P)
        mhalf = const.tile([P, 1], F32, name="mhalf")
        nc.gpsimd.memset(mhalf[:], -0.5)
        swap = const.tile([P, P], F32, name="swap")
        ident_pairs = ident[:].rearrange("p (m e) -> p m e", e=2)
        swap_pairs = swap[:].rearrange("p (m e) -> p m e", e=2)
        for e in range(2):
            nc.gpsimd.tensor_copy(out=swap_pairs[:, :, e], in_=ident_pairs[:, :, 1 - e])
        ident_bf = const.tile([P, P], BF16, name="ident_bf")
        nc.gpsimd.tensor_copy(out=ident_bf[:], in_=ident[:])
        gb = const.tile([P, 3, T], F32, name="gb")
        for i, name in enumerate(("q1_b", "q_gn_g", "q_gn_b")):
            nc.gpsimd.tensor_copy(out=gb[:, i, :], in_=vecs[name][:])

        w1 = const.tile([P, G, 2 * Q_RANK], U8, name="w1", align_bytes=64)
        s1 = const.tile([P, G, Q_RANK], U8, name="s1", align_bytes=64)
        b2 = const.tile([P, 2 * HEADS], F32, name="b2")
        wide, quads, x_codes, y, stats, hw, hq, h_codes, z, u, prods, result, n_bank = {}, {}, {}, {}, {}, {}, {}, {}, {}, {}, {}, {}, {}
        half_done = set()

        def angles():
            for dt in range(2):
                nc.vector.tensor_scalar(out=turns[:, dt, 0, :], in0=pos[:], scalar1=inv[:, dt : dt + 1], scalar2=1.0 / (2 * math.pi), op0=ALU.mult, op1=ALU.mult)
            nc.vector.tensor_scalar(out=turns[:, :, 1, :], in0=turns[:, :, 0, :], scalar1=0.25, scalar2=None, op0=ALU.add)
            turns_flat = turns[:].rearrange("p d k n -> p (d k n)")
            nc.vector.tensor_copy(out=whole[:], in_=turns_flat)
            nc.vector.tensor_tensor(out=frac[:], in0=turns_flat, in1=whole[:], op=ALU.subtract)
            nc.vector.scalar_tensor_tensor(out=wrapped[:].rearrange("p d k n -> p (d k n)"), in0=frac[:], scalar=0.5, in1=frac[:], op0=ALU.is_gt, op1=ALU.subtract)
            for axis, cols in ((0, slice(0, H)), (1, slice(H, H + W))):
                nc.vector.tensor_tensor(
                    out=masked[:, :, :, cols],
                    in0=wrapped[:, :, :, cols],
                    in1=factor[:, :, axis].unsqueeze(1).unsqueeze(3).to_broadcast([P, 2, 2, cols.stop - cols.start]),
                    op=ALU.mult,
                )

        def sines():
            nc.scalar.activation(out=waves[:].rearrange("p k n -> p (k n)"), in_=masked[:].rearrange("p d k n -> p (d k n)"), func=ACT.Sin, scale=-2 * math.pi)

        def tabx(dt):
            nc.vector.tensor_tensor(
                out=table[:, 2 * dt : 2 * dt + 2, :].rearrange("p k (h w) -> p k h w", h=H),
                in0=waves[:, 2 * dt : 2 * dt + 2, 0:H].unsqueeze(3).to_broadcast([P, 2, H, W]),
                in1=waves[:, 2 * dt : 2 * dt + 2, H : H + W].unsqueeze(2).to_broadcast([P, 2, H, W]),
                op=ALU.add,
            )

        def perm(g):
            nc.vector.tensor_copy(out=w1[:, g, :].rearrange("p (t m e) -> p t m e", t=T, e=2), in_=w1_raw[:, g, :].rearrange("p (m t e) -> p t m e", t=T, e=2))
            nc.vector.tensor_copy(out=s1[:, g, :].rearrange("p (t m) -> p t m", t=T), in_=s1_raw[:, g, :].rearrange("p (m t) -> p t m", t=T))

        def widen(b, g, t, on_vector=False):
            if t == 0:
                wide[b, g] = stage.tile([P, T, S], BF16, name="wide", bufs=8)
            src = xb[b, g][:, t * S : (t + 1) * S].bitcast(FP8)
            if on_vector:
                nc.vector.tensor_scalar(out=wide[b, g][:, t, :], in0=src, scalar1=xs[g][:, t : t + 1], scalar2=None, op0=ALU.mult)
            else:
                nc.scalar.activation(out=wide[b, g][:, t, :], in_=src, func=ACT.Copy, scale=xs[g][:, t : t + 1])

        def pile(src, dst):
            banks = []
            for i in range(2):
                bank = psum.tile([P, 256, T], BF16, name="bank")
                for j in range(2):
                    c = 256 * i + 128 * j
                    nc.tensor.matmul(bank[:, 128 * j : 128 * (j + 1), :], lhsT=ident_bf[:], rhs=src[:, :, c : c + 128].rearrange("p t c -> p c t"), start=True, stop=True)
                banks.append(bank)
            for i in range(2):
                nc.scalar.copy(out=dst[:, 256 * i : 256 * (i + 1), :], in_=banks[i][:])

        def ile(b, g):
            quads[b, g] = stage.tile([P, S, T], BF16, name="quads", align_bytes=64)
            if (b, g) in PILED:
                pile(wide[b, g], quads[b, g])
            else:
                nc.vector.tensor_copy(out=quads[b, g][:].rearrange("p (c i) t -> p c t i", i=4), in_=wide[b, g][:].rearrange("p t (c i) -> p c t i", i=4))

        def qnt(b, g):
            codes = keep.tile([P, S], U32, name="codes", align_bytes=64)
            scales = keep.tile([P, S], U8, name="scales", align_bytes=64)
            nc.vector.quantize_mx(out=codes[:].bitcast(FP8X4), scales=scales[:], in_=quads[b, g][:].rearrange("p n t -> p (n t)"))
            x_codes[b, g] = (codes, scales)

        def mm1(b, g):
            codes, scales = x_codes[b, g]
            for t in range(T):
                if g == 0:
                    y[b, t] = psum.tile([P, S], F32, name="bank")
                nc.tensor.matmul_mx(
                    out=y[b, t][:],
                    lhsT=w1[:, g, 256 * t : 256 * (t + 1)].bitcast(FP4X4),
                    lhsT_scale=s1[:, g, P * t : P * (t + 1)],
                    rhs=codes[:].bitcast(FP8X4),
                    rhs_scale=scales[:],
                    start=(g == 0),
                    stop=(g == G - 1),
                )

        def bn(b, t):
            if t == 0:
                stats[b] = {"st": small.tile([P, T, 2, 3], F32, name="st")}
            nc.vector.bn_stats(out=stats[b]["st"][:, t].rearrange("p a b -> p (a b)"), in_=y[b, t][:])

        def tot(b):
            st = stats[b]["st"]
            nc.vector.tensor_tensor(out=st[:, :, :, 1], in0=st[:, :, :, 1], in1=gb[:, 0, :].unsqueeze(2).to_broadcast([P, T, 2]), op=ALU.add)
            ag = small.tile([P, 2], F32, name="ag")
            nc.vector.bn_aggr(out=ag[:], in_=st[:].rearrange("p t a b -> p (t a b)"))
            nc.vector.scalar_tensor_tensor(out=ag[:, 1:2], in0=ag[:, 0:1], scalar=ag[:, 0:1], in1=ag[:, 1:2], op0=ALU.mult, op1=ALU.add)
            total = psum.tile([P, S], F32, name="bank")
            nc.tensor.matmul(total[:, 0:2], lhsT=ones[:], rhs=ag[:], start=True, stop=True)
            stats[b]["total"] = total

        def rstd(b):
            total = stats[b]["total"]
            mu2 = small.tile([P, 1], F32, name="mu2")
            nc.vector.tensor_scalar(out=mu2[:], in0=total[:, 0:1], scalar1=total[:, 0:1], scalar2=None, op0=ALU.mult)
            vare = small.tile([P, 1], F32, name="vare")
            nc.vector.tensor_scalar(out=vare[:], in0=total[:, 1:2], scalar1=mu2[:], scalar2=EPS, op0=ALU.subtract, op1=ALU.add)
            rs = small.tile([P, 1], F32, name="rs")
            nc.gpsimd.tensor_tensor(out=rs[:], in0=vare[:], in1=mhalf[:], op=ALU.pow)
            stats[b]["rs"] = rs

        def aff(b):
            sc = small.tile([P, T], F32, name="sc")
            nc.vector.tensor_scalar(out=sc[:], in0=gb[:, 1, :], scalar1=stats[b]["rs"][:], scalar2=None, op0=ALU.mult)
            bi = small.tile([P, T], F32, name="bi")
            nc.vector.scalar_tensor_tensor(out=bi[:], in0=gb[:, 0, :], scalar=stats[b]["total"][:, 0:1], in1=sc[:], op0=ALU.subtract, op1=ALU.mult)
            bj = small.tile([P, T], F32, name="bj")
            nc.vector.tensor_tensor(out=bj[:], in0=bi[:], in1=gb[:, 2, :], op=ALU.add)
            stats[b]["sc"] = sc
            stats[b]["bi"] = bj

        def nrm(b, t):
            if t == 0:
                hw[b] = stage.tile([P, T, S], BF16, name="hw", bufs=2)
            nc.scalar.activation(out=hw[b][:, t, :], in_=y[b, t][:], func=ACT.Identity, scale=stats[b]["sc"][:, t : t + 1], bias=stats[b]["bi"][:, t : t + 1])

        def hil(b):
            hq[b] = stage.tile([P, S, T], BF16, name="hq", align_bytes=64, bufs=2)
            nc.vector.tensor_copy(out=hq[b][:].rearrange("p (c i) t -> p c t i", i=4), in_=hw[b][:].rearrange("p t (c i) -> p c t i", i=4))

        def hqn(b):
            codes = keep.tile([P, S], U32, name="hcodes", align_bytes=64, bufs=2)
            scales = keep.tile([P, S], U8, name="hscales", align_bytes=64, bufs=2)
            nc.vector.quantize_mx(out=codes[:].bitcast(FP8X4), scales=scales[:], in_=hq[b][:].rearrange("p n t -> p (n t)"))
            h_codes[b] = (codes, scales)

        def bias_columns():
            cols = psum.tile([P, S], F32, name="bank")
            for i in range(2 * HEADS):
                first = HEAD_DIM * (i // 2) + NOPE + P * (i % 2)
                nc.tensor.matmul(cols[:, i : i + 1], lhsT=qb[:, first : first + P], rhs=ones_bf[:, 0:1], start=True, stop=True)
            nc.vector.tensor_copy(out=b2[:], in_=cols[:, 0 : 2 * HEADS])

        def zmm(b, h, dt):
            codes, scales = h_codes[b]
            first = HEAD_DIM * h + NOPE + P * dt
            z[b, h, dt] = psum.tile([P, S], F32, name="bank")
            nc.tensor.matmul_mx(
                out=z[b, h, dt][:],
                lhsT=w2[:, 2 * first : 2 * (first + P)].bitcast(FP4X4),
                lhsT_scale=s2[:, first : first + P],
                rhs=codes[:].bitcast(FP8X4),
                rhs_scale=scales[:],
                start=True,
                stop=True,
            )

        def uu(b, h, dt):
            u[b, h] = stage.tile([P, S], F32, name="u", bufs=3)
            nc.scalar.activation(out=u[b, h][:], in_=z[b, h, dt][:], func=ACT.Identity, bias=b2[:, 2 * h + dt : 2 * h + dt + 1])

        def gab(b, h, dt):
            prod = stage.tile([P, 2, S], F32, name="prod", bufs=6)
            nc.gpsimd.tensor_tensor(out=prod[:], in0=u[b, h][:].unsqueeze(1).to_broadcast([P, 2, S]), in1=table[:, 2 * dt : 2 * dt + 2, :], op=ALU.mult)
            prods[b, h, dt] = prod

        def ab(b, h, dt):
            prod = stage.tile([P, 2, S], F32, name="prod", bufs=6)
            nc.vector.scalar_tensor_tensor(
                out=prod[:],
                in0=z[b, h, dt][:].unsqueeze(1).to_broadcast([P, 2, S]),
                scalar=b2[:, 2 * h + dt : 2 * h + dt + 1],
                in1=table[:, 2 * dt : 2 * dt + 2, :],
                op0=ALU.add,
                op1=ALU.mult,
            )
            prods[b, h, dt] = prod

        def result_half(b, h, half):
            if (b, h) not in result:
                result[b, h] = outs.tile([P, 4, HEAD_DIM], F32, name="result", bufs=4)
            return result[b, h][:, 2 * half : 2 * half + 2]

        def wrote(b, h, half):
            if (b, h, half) in half_done:
                nc.sync.dma_start(out=out[b, h].rearrange("(s p) d -> p s d", p=P)[:, 2 * half : 2 * half + 2], in_=result_half(b, h, half))
            half_done.add((b, h, half))

        def nmm(b, h, half):
            codes, scales = h_codes[b]
            bank = psum.tile([P, 2, NOPE], F32, name="bank")
            for i in range(2):
                st = 2 * half + i
                nc.tensor.matmul_mx(
                    out=bank[:, i, :],
                    lhsT=codes[:, P * st : P * (st + 1)].bitcast(FP8X4),
                    lhsT_scale=scales[:, P * st : P * (st + 1)],
                    rhs=w2[:, 2 * HEAD_DIM * h : 2 * (HEAD_DIM * h + NOPE)].bitcast(FP4X4),
                    rhs_scale=s2[:, HEAD_DIM * h : HEAD_DIM * h + NOPE],
                    start=True,
                    stop=True,
                )
            n_bank[b, h, half] = bank

        def nad(b, h, half):
            nc.vector.tensor_tensor(
                out=result_half(b, h, half)[:, :, 0:NOPE],
                in0=n_bank[b, h, half][:],
                in1=qb[:, HEAD_DIM * h : HEAD_DIM * h + NOPE].unsqueeze(1).to_broadcast([P, 2, NOPE]),
                op=ALU.add,
            )
            wrote(b, h, half)

        def nope1(b, h, half):
            nmm(b, h, half)
            nad(b, h, half)

        def nope(b, h):
            for half in range(2):
                nope1(b, h, half)

        def tail1(b, h, half):
            bank = psum.tile([P, 2, NOPE], F32, name="bank")
            for i in range(2):
                st = 2 * half + i
                for dt in range(2):
                    dst = bank[:, i, P * dt : P * (dt + 1)]
                    nc.tensor.matmul(dst, lhsT=prods[b, h, dt][:, 0, P * st : P * (st + 1)], rhs=ident[:], is_transpose=True, start=True, stop=False)
                    nc.tensor.matmul(dst, lhsT=prods[b, h, dt][:, 1, P * st : P * (st + 1)], rhs=swap[:], is_transpose=True, start=False, stop=True)
            nc.scalar.copy(out=result_half(b, h, half)[:, :, NOPE:HEAD_DIM], in_=bank[:])
            wrote(b, h, half)

        def last_tail(b, h):
            for st in range(4):
                bank = psum.tile([P, NOPE], F32, name="bank")
                for dt in range(2):
                    dst = bank[:, P * dt : P * (dt + 1)]
                    nc.tensor.matmul(dst, lhsT=prods[b, h, dt][:, 0, P * st : P * (st + 1)], rhs=ident[:], is_transpose=True, start=True, stop=False)
                    nc.tensor.matmul(dst, lhsT=prods[b, h, dt][:, 1, P * st : P * (st + 1)], rhs=swap[:], is_transpose=True, start=False, stop=True)
                piece = result[b, h][:, st]
                if st % 2 == 0:
                    nc.scalar.copy(out=piece[:, NOPE:HEAD_DIM], in_=bank[:])
                else:
                    nc.vector.tensor_copy(out=piece[:, NOPE:HEAD_DIM], in_=bank[:])
                nc.sync.dma_start(out=out[b, h].rearrange("(s p) d -> p s d", p=P)[:, st], in_=piece)

        def tail(b, h):
            for half in range(2):
                tail1(b, h, half)

        angles()
        for t in range(2):
            widen(0, 0, t)
        for t in range(2, T):
            widen(0, 0, t, on_vector=True)
        for g in range(1, G):
            for t in range(T):
                widen(0, g, t)
        sines()
        ile(0, 0)
        perm(0)
        qnt(0, 0)
        mm1(0, 0)
        perm(1)
        ile(0, 1)
        perm(2)
        ile(0, 2)
        qnt(0, 1)
        mm1(0, 1)
        qnt(0, 2)
        mm1(0, 2)
        ile(0, 3)
        perm(3)
        qnt(0, 3)
        mm1(0, 3)
        ahead = [(g, t) for g in range(G) for t in range(T)]
        for g, t in ahead[:14]:
            widen(1, g, t)
        for t in range(T):
            bn(0, t)
        tot(0)
        ile(1, 0)
        rstd(0)
        tabx(0)
        ile(1, 1)
        for g, t in ahead[14:]:
            widen(1, g, t)
        qnt(1, 0)
        aff(0)
        for t in range(T):
            nrm(0, t)
        ile(1, 2)
        qnt(1, 1)
        mm1(1, 0)
        mm1(1, 1)
        ile(1, 3)
        bias_columns()
        hil(0)
        qnt(1, 2)
        hqn(0)
        tabx(1)
        qnt(1, 3)
        zmm(0, 0, 0)
        zmm(0, 0, 1)
        mm1(1, 2)
        mm1(1, 3)
        uu(0, 0, 1)
        ab(0, 0, 0)
        nmm(0, 0, 0)
        zmm(0, 1, 1)
        nmm(0, 0, 1)
        for t in range(T):
            bn(1, t)
        uu(0, 1, 1)
        tot(1)
        gab(0, 0, 1)
        rstd(1)
        nad(0, 0, 0)
        aff(1)
        for t in range(T):
            nrm(1, t)
        nad(0, 0, 1)
        zmm(0, 1, 0)
        nmm(0, 1, 0)
        tail(0, 0)
        ab(0, 1, 0)
        gab(0, 1, 1)
        nad(0, 1, 0)
        hil(1)
        hqn(1)
        zmm(0, 2, 1)
        uu(0, 2, 1)
        gab(0, 2, 1)
        nope1(0, 1, 1)
        zmm(0, 2, 0)
        ab(0, 2, 0)
        tail(0, 1)
        zmm(0, 3, 1)
        uu(0, 3, 1)
        gab(0, 3, 1)
        nope(0, 2)
        zmm(0, 3, 0)
        ab(0, 3, 0)
        zmm(1, 0, 1)
        uu(1, 0, 1)
        gab(1, 0, 1)
        zmm(1, 0, 0)
        tail(0, 2)
        last = (0, 3)
        for h in range(HEADS):
            ab(1, h, 0)
            if h < 3:
                zmm(1, h + 1, 1)
                uu(1, h + 1, 1)
                gab(1, h + 1, 1)
                zmm(1, h + 1, 0)
            nope(*last)
            if h == HEADS - 1:
                nope(1, h)
            tail(*last)
            last = (1, h)
        last_tail(*last)
